import numpy as np
import ml_dtypes


def mxq(x, axis, fmt="e4m3"):
    dtype, down = {"e4m3": (ml_dtypes.float8_e4m3fn, 7), "e5m2": (ml_dtypes.float8_e5m2, 14)}[fmt]
    v = np.moveaxis(np.asarray(x, np.float32).astype(ml_dtypes.bfloat16).astype(np.float64), axis, -1)
    blocks = v.reshape(v.shape[:-1] + (-1, 32))
    amax = np.abs(blocks).max(-1, keepdims=True)
    byte = np.maximum(np.where(amax > 0, np.frexp(amax)[1] - 1 + 127, 0) - down, 1)
    scale = np.exp2(byte - 127.0)
    codes = (blocks / scale).astype(np.float32).astype(dtype).astype(np.float64)
    return np.moveaxis((codes * scale).reshape(v.shape), -1, axis)


WIDE = False


def mx_kscale(k):
    if not WIDE:
        return np.ones(k)
    levels = np.array([10, -10, 5, -5, 0])
    a = np.random.permutation(np.resize(levels, k // 512 * 4)).reshape(k // 512, 4)
    idx = np.arange(k)
    return np.exp2(a[idx // 512, idx % 128 // 32])


BF16 = ml_dtypes.bfloat16


def bf(x):
    return np.asarray(x, np.float32).astype(BF16)


def f64(x):
    return np.asarray(x).astype(np.float64)


E2M1 = np.array([0.0, 0.5, 1.0, 1.5, 2.0, 3.0, 4.0, 6.0, -0.0, -0.5, -1.0, -1.5, -2.0, -3.0, -4.0, -6.0])


def pack_weight(w, fmt):
    k, n = w.shape
    w = f64(bf(w)).reshape(k // 32, 32, n)
    amax = np.abs(w).max(1)
    if fmt == "e4m3":
        byte = np.frexp(amax)[1] - 1 + 127 - 7
    else:
        mant, ex = np.frexp(amax / 6.0)
        byte = np.where(mant > 0.5, ex, ex - 1) + 127
    byte = np.clip(np.where(amax > 0, byte, 1), 1, 254)
    scaled = (w * np.exp2(127.0 - byte)[:, None, :]).reshape(k, n).astype(np.float32)
    by_word = np.ascontiguousarray(scaled.reshape(k // 512, 128, 4, n).transpose(0, 1, 3, 2))
    if fmt == "e4m3":
        words = by_word.astype(ml_dtypes.float8_e4m3fn).view(np.uint8)
    else:
        c = by_word.astype(ml_dtypes.float4_e2m1fn).view(np.uint8) & 0xF
        words = c[..., 0::2] | (c[..., 1::2] << 4)
    return np.ascontiguousarray(words), np.ascontiguousarray(byte.astype(np.uint8).reshape(k // 512, 16, n))


def unpack_weight(words, scales, fmt):
    g, p, n, _ = words.shape
    if fmt == "e4m3":
        vals = np.ascontiguousarray(words).view(ml_dtypes.float8_e4m3fn).astype(np.float64)
    else:
        nib = np.empty((g, p, n, 4), np.uint8)
        nib[..., 0::2] = words & 0xF
        nib[..., 1::2] = words >> 4
        vals = E2M1[nib]
    vals = vals * np.repeat(np.exp2(scales.astype(np.float64) - 127.0), 8, axis=1)[..., None]
    return vals.transpose(0, 1, 3, 2).reshape(g * 512, n)


B, S, D, F = 2, 256, 1024, 2560


def silu(v):
    return v / (1.0 + np.exp(-v))


def setup_inputs():
    s, t = mx_kscale(D), mx_kscale(F)
    x = bf(np.random.standard_normal((B, S, D)) * s)
    gate_words, gate_scales = pack_weight((np.random.standard_normal((F, D)) * 1.0 / np.sqrt(D) / s[None, :]).T, "e4m3")
    up_words, up_scales = pack_weight((np.random.standard_normal((F, D)) * 1.0 / np.sqrt(D) / s[None, :] * t[:, None]).T, "e4m3")
    down_words, down_scales = pack_weight((np.random.standard_normal((D, F)) * 2.0 / np.sqrt(F) / t[None, :]).T, "e4m3")
    return {"x": x,
            "W_gate_words": gate_words, "W_gate_scales": gate_scales,
            "W_up_words": up_words, "W_up_scales": up_scales,
            "W_down_words": down_words, "W_down_scales": down_scales}


def reference(x, W_gate_words, W_gate_scales, W_up_words, W_up_scales, W_down_words, W_down_scales):
    out_shape = x.shape[:-1] + (W_down_words.shape[2],)
    xf = f64(x).reshape(-1, x.shape[-1])
    xq = mxq(xf, 1, "e4m3")
    up = xq @ unpack_weight(W_up_words, W_up_scales, "e4m3")
    gate = silu(xq @ unpack_weight(W_gate_words, W_gate_scales, "e4m3"))
    h = gate * up
    y = mxq(h, 1, "e4m3") @ unpack_weight(W_down_words, W_down_scales, "e4m3")
    return y.reshape(out_shape)

@@ -1,0 +1,259 @@
+from contextlib import ExitStack
+
+import concourse.mybir as mybir
+from concourse.masks import make_identity
+
+BF16 = mybir.dt.bfloat16
+F32 = mybir.dt.float32
+I32 = mybir.dt.int32
+U32 = mybir.dt.uint32
+U8 = mybir.dt.uint8
+FP8X4 = mybir.dt.float8_e4m3fn_x4
+
+P = 128
+PACK = 4
+K_PASS = P * PACK
+N_TILE = 512
+
+TOKENS = 512
+D_MODEL = 1024
+D_FF = 2560
+
+TOKEN_TILES = TOKENS // P
+X_PASSES = D_MODEL // K_PASS
+FF_CHUNKS = D_FF // N_TILE
+OUT_HALVES = D_MODEL // N_TILE
+
+QUADRANTS = 4
+PLANE_ROWS = 4
+PLANES_PER_TILE = 4
+
+UNITS_BEFORE_TRANSPOSES = 2
+TILES_PER_ROUND = 2
+
+FLOPS = 2 * TOKENS * D_MODEL * D_FF * 3
+
+
+def tile_mixllamamlp_kernel(
+    tc, x, W_gate_words, W_gate_scales, W_up_words, W_up_scales, W_down_words, W_down_scales, out
+):
+    nc = tc.nc
+    x_rows = x.flatten_outer_dims()
+    out_rows = out.flatten_outer_dims()
+
+    with ExitStack() as ctx:
+        resident = ctx.enter_context(tc.tile_pool(name="resident", bufs=1))
+        x_stage = ctx.enter_context(tc.tile_pool(name="x_stage", bufs=2))
+        silu_pool = ctx.enter_context(tc.tile_pool(name="silu_pool", bufs=3))
+        h_stage = ctx.enter_context(tc.tile_pool(name="h_stage", bufs=2))
+        y_pool = ctx.enter_context(tc.tile_pool(name="y_pool", bufs=4))
+        mx_banks = ctx.enter_context(tc.psum_pool(name="mx_banks", bufs=6))
+        tr_banks = ctx.enter_context(tc.psum_pool(name="tr_banks", bufs=2))
+        ctx.enter_context(tc.manual_schedule())
+
+        gate_up_planes = resident.tile([P, D_FF], U8, align_bytes=64)
+        down_planes = resident.tile([P, 2, D_MODEL], U8, align_bytes=64)
+        nc.vector.memset(gate_up_planes[:].bitcast(I32), 0)
+        nc.vector.memset(down_planes[:].rearrange("p s n -> p (s n)").bitcast(I32), 0)
+
+        table_warmer = resident.tile([P, 1], F32)
+        nc.vector.memset(table_warmer[:], 0.0)
+        nc.scalar.activation(out=table_warmer[:], in_=table_warmer[:], func=mybir.ActivationFunctionType.Silu)
+
+        identity_f32 = resident.tile([P, P], F32)
+        make_identity(nc, identity_f32[:])
+        identity_bf16 = resident.tile([P, P], BF16)
+        make_identity(nc, identity_bf16[:])
+
+        x_tiles = []
+        for m in range(TOKEN_TILES):
+            x_tile = resident.tile([P, D_MODEL], BF16, name="x_tile_%d" % m)
+            nc.sync.dma_start(out=x_tile[:], in_=x_rows[m * P : (m + 1) * P, :])
+            x_tiles.append(x_tile)
+
+        for quadrant in range(QUADRANTS):
+            for w, scales in enumerate((W_gate_scales, W_up_scales)):
+                first = 32 * quadrant + PLANE_ROWS * X_PASSES * w
+                nc.sync.dma_start(
+                    out=gate_up_planes[first : first + PLANE_ROWS * X_PASSES, :].bitcast(I32),
+                    in_=scales[:, PLANE_ROWS * quadrant : PLANE_ROWS * (quadrant + 1), :].bitcast(I32),
+                )
+
+        gate_up_words = []
+        for c in range(FF_CHUNKS):
+            pair = []
+            for w, words in enumerate((W_gate_words, W_up_words)):
+                chunk_words = resident.tile([P, X_PASSES, N_TILE], I32, name="words_%d_%d" % (c, w), align_bytes=64)
+                nc.sync.dma_start(
+                    out=chunk_words[:],
+                    in_=words.rearrange("g p n t -> p g (n t)").bitcast(I32)[:, :, c * N_TILE : (c + 1) * N_TILE],
+                )
+                pair.append(chunk_words)
+            gate_up_words.append(pair)
+
+        for quadrant in range(QUADRANTS):
+            rows = slice(PLANE_ROWS * quadrant, PLANE_ROWS * (quadrant + 1))
+            nc.sync.dma_start(
+                out=down_planes[32 * quadrant : 32 * quadrant + PLANE_ROWS * PLANES_PER_TILE, 0, :].bitcast(I32),
+                in_=W_down_scales[0:PLANES_PER_TILE, rows, :].bitcast(I32),
+            )
+            nc.sync.dma_start(
+                out=down_planes[32 * quadrant : 32 * quadrant + PLANE_ROWS, 1, :].bitcast(I32),
+                in_=W_down_scales[PLANES_PER_TILE, rows, :].bitcast(I32),
+            )
+
+        down_words = []
+        for g in range(FF_CHUNKS):
+            pass_words = resident.tile([P, D_MODEL], I32, name="down_words_%d" % g, align_bytes=64)
+            nc.sync.dma_start(out=pass_words[:], in_=W_down_words[g].rearrange("p n t -> p (n t)").bitcast(I32))
+            down_words.append(pass_words)
+
+        x_codes = resident.tile([P, TOKEN_TILES, X_PASSES, P], U32, align_bytes=64)
+        x_scales = resident.tile([P, TOKEN_TILES, X_PASSES, P], U8, align_bytes=64)
+        x_grouped = {}
+
+        def transpose_x(m):
+            x_words = x_tiles[m][:].bitcast(F32)
+            bank = tr_banks.tile([P, X_PASSES * 2, P], F32, tag="tr")
+            for g in range(X_PASSES):
+                for u in range(2):
+                    nc.tensor.transpose(
+                        out=bank[:, 2 * g + u, :],
+                        in_=x_words[:, 256 * g + u : 256 * (g + 1) : 2],
+                        identity=identity_f32[:],
+                    )
+            grouped = x_stage.tile([P, X_PASSES, P, PACK], BF16, align_bytes=64)
+            grouped_words = (
+                grouped[:]
+                .rearrange("p g r t -> p (g r t)")
+                .bitcast(F32)
+                .rearrange("p (g r u) -> p g r u", g=X_PASSES, u=2)
+            )
+            transposed = bank[:].rearrange("p (g u) r -> p g r u", u=2)
+            if m % 2 == 0:
+                nc.vector.tensor_copy(out=grouped_words, in_=transposed)
+            else:
+                nc.scalar.copy(out=grouped_words, in_=transposed)
+            x_grouped[m] = grouped
+
+        def quantise_x(m):
+            nc.vector.quantize_mx(
+                out=x_codes[:, m, :, :].rearrange("p g r -> p (g r)").bitcast(FP8X4),
+                scales=x_scales[:, m, :, :].rearrange("p g r -> p (g r)"),
+                in_=x_grouped[m][:].rearrange("p g r t -> p (g r t)"),
+            )
+
+        for m in range(TOKEN_TILES):
+            transpose_x(m)
+            if m > 0:
+                quantise_x(m - 1)
+        quantise_x(TOKEN_TILES - 1)
+
+        h_codes = resident.tile([P, FF_CHUNKS, TOKENS], U32, align_bytes=64)
+        h_scales = resident.tile([P, FF_CHUNKS, TOKENS], U8, align_bytes=64)
+        h_sorted = {}
+        h_grouped = {}
+
+        def project(w, c, m):
+            bank = mx_banks.tile([P, N_TILE], F32, tag="mx")
+            for g in range(X_PASSES):
+                plane_start = PLANE_ROWS * (X_PASSES * w + g)
+                nc.tensor.matmul_mx(
+                    out=bank[:],
+                    lhsT=x_codes[:, m, g, :].bitcast(FP8X4),
+                    lhsT_scale=x_scales[:, m, g, :],
+                    rhs=gate_up_words[c][w][:, g, :].bitcast(FP8X4),
+                    rhs_scale=gate_up_planes[plane_start:P, c * N_TILE : (c + 1) * N_TILE],
+                    start=(g == 0),
+                    stop=(g == X_PASSES - 1),
+                )
+            return bank
+
+        def gate_up_unit(c, m):
+            gate_bank = project(0, c, m)
+            up_bank = project(1, c, m)
+            silu_gate = silu_pool.tile([P, PACK, P], F32)
+            nc.scalar.activation(
+                out=silu_gate[:],
+                in_=gate_bank[:].rearrange("r (p t) -> r t p", t=PACK),
+                func=mybir.ActivationFunctionType.Silu,
+            )
+            nc.vector.tensor_tensor(
+                out=h_sorted[c][:, m, :, :],
+                in0=up_bank[:].rearrange("r (p t) -> r t p", t=PACK),
+                in1=silu_gate[:],
+                op=mybir.AluOpType.mult,
+            )
+
+        def transpose_h(c):
+            grouped = h_stage.tile([P, TOKEN_TILES, P, PACK], BF16, align_bytes=64)
+            for half in range(2):
+                bank = tr_banks.tile([P, 2, PACK, P], BF16, tag="tr")
+                for i in range(2):
+                    for t in range(PACK):
+                        nc.tensor.transpose(
+                            out=bank[:, i, t, :],
+                            in_=h_sorted[c][:, 2 * half + i, t, :],
+                            identity=identity_bf16[:],
+                        )
+                transposed = bank[:].rearrange("p i t r -> p i r t")
+                if half == 0:
+                    nc.scalar.copy(out=grouped[:, 0:2, :, :], in_=transposed)
+                else:
+                    nc.vector.tensor_copy(out=grouped[:, 2:4, :, :], in_=transposed)
+            h_grouped[c] = grouped
+
+        def quantise_h(c):
+            nc.vector.quantize_mx(
+                out=h_codes[:, c, :].bitcast(FP8X4),
+                scales=h_scales[:, c, :],
+                in_=h_grouped[c][:].rearrange("p m r t -> p (m r t)"),
+            )
+
+        for c in range(FF_CHUNKS):
+            h_sorted[c] = h_stage.tile([P, TOKEN_TILES, PACK, P], BF16, name="h_sorted")
+            for m in range(TOKEN_TILES):
+                gate_up_unit(c, m)
+                if c > 0 and m + 1 == UNITS_BEFORE_TRANSPOSES:
+                    transpose_h(c - 1)
+                if c > 0 and m == UNITS_BEFORE_TRANSPOSES:
+                    quantise_h(c - 1)
+
+        def down_pass(bank, m, half, g):
+            if g < PLANES_PER_TILE:
+                plane = down_planes[PLANE_ROWS * g : P, 0, half * N_TILE : (half + 1) * N_TILE]
+            else:
+                plane = down_planes[:, 1, half * N_TILE : (half + 1) * N_TILE]
+            nc.tensor.matmul_mx(
+                out=bank[:],
+                lhsT=h_codes[:, g, m * P : (m + 1) * P].bitcast(FP8X4),
+                lhsT_scale=h_scales[:, g, m * P : (m + 1) * P],
+                rhs=down_words[g][:, half * N_TILE : (half + 1) * N_TILE].bitcast(FP8X4),
+                rhs_scale=plane,
+                start=(g == 0),
+                stop=(g == FF_CHUNKS - 1),
+            )
+
+        last = FF_CHUNKS - 1
+        for first_tile in range(0, TOKEN_TILES, TILES_PER_ROUND):
+            open_banks = []
+            for m in range(first_tile, first_tile + TILES_PER_ROUND):
+                for half in range(OUT_HALVES):
+                    bank = mx_banks.tile([P, N_TILE], F32, tag="mx")
+                    for g in range(last):
+                        down_pass(bank, m, half, g)
+                    open_banks.append((bank, m, half))
+                    if first_tile == 0 and len(open_banks) == 1:
+                        transpose_h(last)
+                    if first_tile == 0 and len(open_banks) == 2:
+                        quantise_h(last)
+            for bank, m, half in open_banks:
+                down_pass(bank, m, half, last)
+                y_tile = y_pool.tile([P, N_TILE], F32)
+                if half == 0:
+                    nc.vector.tensor_copy(out=y_tile[:], in_=bank[:])
+                else:
+                    nc.scalar.copy(out=y_tile[:], in_=bank[:])
+                nc.sync.dma_start(
+                    out=out_rows[m * P : (m + 1) * P, half * N_TILE : (half + 1) * N_TILE], in_=y_tile[:]
+                )

@@ -21,15 +21,23 @@ D_FF = 2560
 
 TOKEN_TILES = TOKENS // P
 X_PASSES = D_MODEL // K_PASS
-FF_CHUNKS = D_FF // N_TILE
+FF_CHUNKS = D_FF // K_PASS
+TILES_PER_CHUNK = K_PASS // P
+FEATURE_TILES = D_FF // P
 OUT_HALVES = D_MODEL // N_TILE
 
 QUADRANTS = 4
+QUADRANT = 32
 PLANE_ROWS = 4
 PLANES_PER_TILE = 4
 
-UNITS_BEFORE_TRANSPOSES = 2
-TILES_PER_ROUND = 2
+PIECE = 256
+TILES_PER_PIECE = PIECE // P
+PIECES = D_FF // PIECE
+PIECES_UP_FRONT = 4
+
+VECTOR_SHARE = 320
+EARLY_BANKS = 5
 
 FLOPS = 2 * TOKENS * D_MODEL * D_FF * 3
 
@@ -43,12 +51,11 @@ def tile_mixllamamlp_kernel(
 
     with ExitStack() as ctx:
         resident = ctx.enter_context(tc.tile_pool(name="resident", bufs=1))
-        x_stage = ctx.enter_context(tc.tile_pool(name="x_stage", bufs=2))
+        x_stage = ctx.enter_context(tc.tile_pool(name="x_stage", bufs=4))
         silu_pool = ctx.enter_context(tc.tile_pool(name="silu_pool", bufs=3))
         h_stage = ctx.enter_context(tc.tile_pool(name="h_stage", bufs=2))
         y_pool = ctx.enter_context(tc.tile_pool(name="y_pool", bufs=4))
-        mx_banks = ctx.enter_context(tc.psum_pool(name="mx_banks", bufs=6))
-        tr_banks = ctx.enter_context(tc.psum_pool(name="tr_banks", bufs=2))
+        banks = ctx.enter_context(tc.psum_pool(name="banks", bufs=8))
         ctx.enter_context(tc.manual_schedule())
 
         gate_up_planes = resident.tile([P, D_FF], U8, align_bytes=64)
@@ -62,8 +69,6 @@ def tile_mixllamamlp_kernel(
 
         identity_f32 = resident.tile([P, P], F32)
         make_identity(nc, identity_f32[:])
-        identity_bf16 = resident.tile([P, P], BF16)
-        make_identity(nc, identity_bf16[:])
 
         x_tiles = []
         for m in range(TOKEN_TILES):
@@ -73,48 +78,65 @@ def tile_mixllamamlp_kernel(
 
         for quadrant in range(QUADRANTS):
             for w, scales in enumerate((W_gate_scales, W_up_scales)):
-                first = 32 * quadrant + PLANE_ROWS * X_PASSES * w
+                first = QUADRANT * quadrant + PLANE_ROWS * X_PASSES * w
                 nc.sync.dma_start(
                     out=gate_up_planes[first : first + PLANE_ROWS * X_PASSES, :].bitcast(I32),
                     in_=scales[:, PLANE_ROWS * quadrant : PLANE_ROWS * (quadrant + 1), :].bitcast(I32),
                 )
 
-        gate_up_words = []
-        for c in range(FF_CHUNKS):
-            pair = []
-            for w, words in enumerate((W_gate_words, W_up_words)):
-                chunk_words = resident.tile([P, X_PASSES, N_TILE], I32, name="words_%d_%d" % (c, w), align_bytes=64)
-                nc.sync.dma_start(
-                    out=chunk_words[:],
-                    in_=words.rearrange("g p n t -> p g (n t)").bitcast(I32)[:, :, c * N_TILE : (c + 1) * N_TILE],
-                )
-                pair.append(chunk_words)
-            gate_up_words.append(pair)
+        gate_up_words = {}
 
-        for quadrant in range(QUADRANTS):
+        def load_gate_up_piece(piece, w):
+            words = (W_gate_words, W_up_words)[w]
+            piece_words = resident.tile([P, X_PASSES, PIECE], I32, name="words_%d_%d" % (piece, w), align_bytes=64)
+            nc.sync.dma_start(
+                out=piece_words[:],
+                in_=words.rearrange("g p n t -> p g (n t)").bitcast(I32)[:, :, piece * PIECE : (piece + 1) * PIECE],
+            )
+            gate_up_words[piece, w] = piece_words
+
+        def load_down_planes(quadrant):
             rows = slice(PLANE_ROWS * quadrant, PLANE_ROWS * (quadrant + 1))
             nc.sync.dma_start(
-                out=down_planes[32 * quadrant : 32 * quadrant + PLANE_ROWS * PLANES_PER_TILE, 0, :].bitcast(I32),
+                out=down_planes[QUADRANT * quadrant : QUADRANT * quadrant + PLANE_ROWS * PLANES_PER_TILE, 0, :].bitcast(I32),
                 in_=W_down_scales[0:PLANES_PER_TILE, rows, :].bitcast(I32),
             )
             nc.sync.dma_start(
-                out=down_planes[32 * quadrant : 32 * quadrant + PLANE_ROWS, 1, :].bitcast(I32),
+                out=down_planes[QUADRANT * quadrant : QUADRANT * quadrant + PLANE_ROWS, 1, :].bitcast(I32),
                 in_=W_down_scales[PLANES_PER_TILE, rows, :].bitcast(I32),
             )
 
-        down_words = []
-        for g in range(FF_CHUNKS):
+        down_words = {}
+
+        def load_down_words(g):
             pass_words = resident.tile([P, D_MODEL], I32, name="down_words_%d" % g, align_bytes=64)
             nc.sync.dma_start(out=pass_words[:], in_=W_down_words[g].rearrange("p n t -> p (n t)").bitcast(I32))
-            down_words.append(pass_words)
+            down_words[g] = pass_words
 
-        x_codes = resident.tile([P, TOKEN_TILES, X_PASSES, P], U32, align_bytes=64)
-        x_scales = resident.tile([P, TOKEN_TILES, X_PASSES, P], U8, align_bytes=64)
+        for piece in range(PIECES_UP_FRONT):
+            load_gate_up_piece(piece, 0)
+            load_gate_up_piece(piece, 1)
+
+        def load_behind_tile(i):
+            later = 2 * (PIECES - PIECES_UP_FRONT)
+            if i < later:
+                load_gate_up_piece(PIECES_UP_FRONT + i // 2, i % 2)
+            elif i < later + 2:
+                load_down_planes(2 * (i - later))
+                load_down_planes(2 * (i - later) + 1)
+            elif i < later + 5:
+                load_down_words(i - later - 2)
+            elif i == FEATURE_TILES - 1:
+                load_down_words(3)
+                load_down_words(4)
+
+        x_codes = resident.tile([P, X_PASSES, TOKENS], U32, align_bytes=64)
+        x_scales = resident.tile([P, X_PASSES, TOKENS], U8, align_bytes=64)
         x_grouped = {}
 
         def transpose_x(m):
             x_words = x_tiles[m][:].bitcast(F32)
-            bank = tr_banks.tile([P, X_PASSES * 2, P], F32, tag="tr")
+            bank = banks.tile([P, X_PASSES * 2, P], F32, tag="bank")
             for g in range(X_PASSES):
                 for u in range(2):
                     nc.tensor.transpose(
@@ -137,11 +159,12 @@ def tile_mixllamamlp_kernel(
             x_grouped[m] = grouped
 
         def quantise_x(m):
-            nc.vector.quantize_mx(
-                out=x_codes[:, m, :, :].rearrange("p g r -> p (g r)").bitcast(FP8X4),
-                scales=x_scales[:, m, :, :].rearrange("p g r -> p (g r)"),
-                in_=x_grouped[m][:].rearrange("p g r t -> p (g r t)"),
-            )
+            for g in range(X_PASSES):
+                nc.vector.quantize_mx(
+                    out=x_codes[:, g, m * P : (m + 1) * P].bitcast(FP8X4),
+                    scales=x_scales[:, g, m * P : (m + 1) * P],
+                    in_=x_grouped[m][:, g, :, :].rearrange("p r t -> p (r t)"),
+                )
 
         for m in range(TOKEN_TILES):
             transpose_x(m)
@@ -151,73 +174,67 @@ def tile_mixllamamlp_kernel(
 
         h_codes = resident.tile([P, FF_CHUNKS, TOKENS], U32, align_bytes=64)
         h_scales = resident.tile([P, FF_CHUNKS, TOKENS], U8, align_bytes=64)
+        h_rows = {}
         h_sorted = {}
         h_grouped = {}
 
-        def project(w, c, m):
-            bank = mx_banks.tile([P, N_TILE], F32, tag="mx")
+        def project(w, i):
+            bank = banks.tile([P, TOKENS], F32, tag="bank")
+            piece, place = divmod(i, TILES_PER_PIECE)
             for g in range(X_PASSES):
                 plane_start = PLANE_ROWS * (X_PASSES * w + g)
                 nc.tensor.matmul_mx(
                     out=bank[:],
-                    lhsT=x_codes[:, m, g, :].bitcast(FP8X4),
-                    lhsT_scale=x_scales[:, m, g, :],
-                    rhs=gate_up_words[c][w][:, g, :].bitcast(FP8X4),
-                    rhs_scale=gate_up_planes[plane_start:P, c * N_TILE : (c + 1) * N_TILE],
+                    lhsT=gate_up_words[piece, w][:, g, place * P : (place + 1) * P].bitcast(FP8X4),
+                    lhsT_scale=gate_up_planes[plane_start:P, i * P : (i + 1) * P],
+                    rhs=x_codes[:, g, :].bitcast(FP8X4),
+                    rhs_scale=x_scales[:, g, :],
                     start=(g == 0),
                     stop=(g == X_PASSES - 1),
                 )
             return bank
 
-        def gate_up_unit(c, m):
-            gate_bank = project(0, c, m)
-            up_bank = project(1, c, m)
-            silu_gate = silu_pool.tile([P, PACK, P], F32)
-            nc.scalar.activation(
-                out=silu_gate[:],
-                in_=gate_bank[:].rearrange("r (p t) -> r t p", t=PACK),
-                func=mybir.ActivationFunctionType.Silu,
-            )
+        def feature_tile(c, j):
+            i = TILES_PER_CHUNK * c + j
+            gate_bank = project(0, i)
+            up_bank = project(1, i)
+            silu_gate = silu_pool.tile([P, TOKENS], F32)
+            nc.scalar.activation(out=silu_gate[:], in_=gate_bank[:], func=mybir.ActivationFunctionType.Silu)
             nc.vector.tensor_tensor(
-                out=h_sorted[c][:, m, :, :],
-                in0=up_bank[:].rearrange("r (p t) -> r t p", t=PACK),
-                in1=silu_gate[:],
-                op=mybir.AluOpType.mult,
+                out=h_rows[c][:, j, :], in0=up_bank[:], in1=silu_gate[:], op=mybir.AluOpType.mult
             )
+            for t in range(PACK):
+                nc.sync.dma_start(
+                    out=h_sorted[c][QUADRANT * j : QUADRANT * (j + 1), t, :], in_=h_rows[c][t:P:PACK, j, :]
+                )
 
-        def transpose_h(c):
-            grouped = h_stage.tile([P, TOKEN_TILES, P, PACK], BF16, align_bytes=64)
-            for half in range(2):
-                bank = tr_banks.tile([P, 2, PACK, P], BF16, tag="tr")
-                for i in range(2):
-                    for t in range(PACK):
-                        nc.tensor.transpose(
-                            out=bank[:, i, t, :],
-                            in_=h_sorted[c][:, 2 * half + i, t, :],
-                            identity=identity_bf16[:],
-                        )
-                transposed = bank[:].rearrange("p i t r -> p i r t")
-                if half == 0:
-                    nc.scalar.copy(out=grouped[:, 0:2, :, :], in_=transposed)
-                else:
-                    nc.vector.tensor_copy(out=grouped[:, 2:4, :, :], in_=transposed)
+        def group_h(c):
+            grouped = h_stage.tile([P, TOKENS, PACK], BF16, align_bytes=64, name="h_grouped")
+            by_token = h_sorted[c][:].rearrange("p t r -> p r t")
+            nc.vector.tensor_copy(out=grouped[:, 0:VECTOR_SHARE, :], in_=by_token[:, 0:VECTOR_SHARE, :])
+            nc.scalar.copy(out=grouped[:, VECTOR_SHARE:TOKENS, :], in_=by_token[:, VECTOR_SHARE:TOKENS, :])
             h_grouped[c] = grouped
 
         def quantise_h(c):
             nc.vector.quantize_mx(
                 out=h_codes[:, c, :].bitcast(FP8X4),
                 scales=h_scales[:, c, :],
-                in_=h_grouped[c][:].rearrange("p m r t -> p (m r t)"),
+                in_=h_grouped[c][:].rearrange("p r t -> p (r t)"),
             )
 
         for c in range(FF_CHUNKS):
-            h_sorted[c] = h_stage.tile([P, TOKEN_TILES, PACK, P], BF16, name="h_sorted")
-            for m in range(TOKEN_TILES):
-                gate_up_unit(c, m)
-                if c > 0 and m + 1 == UNITS_BEFORE_TRANSPOSES:
-                    transpose_h(c - 1)
-                if c > 0 and m == UNITS_BEFORE_TRANSPOSES:
+            h_rows[c] = h_stage.tile([P, TILES_PER_CHUNK, TOKENS], BF16, name="h_rows")
+            h_sorted[c] = h_stage.tile([P, PACK, TOKENS], BF16, name="h_sorted")
+            for j in range(TILES_PER_CHUNK):
+                feature_tile(c, j)
+                load_behind_tile(TILES_PER_CHUNK * c + j)
+                if c > 0 and j == 2:
+                    group_h(c - 1)
+                if c > 0 and j == 3:
                     quantise_h(c - 1)
+        last = FF_CHUNKS - 1
+        group_h(last)
+        quantise_h(last)
 
         def down_pass(bank, m, half, g):
             if g < PLANES_PER_TILE:
@@ -234,26 +251,27 @@ def tile_mixllamamlp_kernel(
                 stop=(g == FF_CHUNKS - 1),
             )
 
-        last = FF_CHUNKS - 1
-        for first_tile in range(0, TOKEN_TILES, TILES_PER_ROUND):
-            open_banks = []
-            for m in range(first_tile, first_tile + TILES_PER_ROUND):
-                for half in range(OUT_HALVES):
-                    bank = mx_banks.tile([P, N_TILE], F32, tag="mx")
-                    for g in range(last):
-                        down_pass(bank, m, half, g)
-                    open_banks.append((bank, m, half))
-                    if first_tile == 0 and len(open_banks) == 1:
-                        transpose_h(last)
-                    if first_tile == 0 and len(open_banks) == 2:
-                        quantise_h(last)
-            for bank, m, half in open_banks:
-                down_pass(bank, m, half, last)
-                y_tile = y_pool.tile([P, N_TILE], F32)
-                if half == 0:
-                    nc.vector.tensor_copy(out=y_tile[:], in_=bank[:])
-                else:
-                    nc.scalar.copy(out=y_tile[:], in_=bank[:])
-                nc.sync.dma_start(
-                    out=out_rows[m * P : (m + 1) * P, half * N_TILE : (half + 1) * N_TILE], in_=y_tile[:]
-                )
+        def store(bank, m, half):
+            y_tile = y_pool.tile([P, N_TILE], F32)
+            if half == 0:
+                nc.vector.tensor_copy(out=y_tile[:], in_=bank[:])
+            else:
+                nc.scalar.copy(out=y_tile[:], in_=bank[:])
+            nc.sync.dma_start(out=out_rows[m * P : (m + 1) * P, half * N_TILE : (half + 1) * N_TILE], in_=y_tile[:])
+
+        outputs = [(m, half) for m in range(TOKEN_TILES) for half in range(OUT_HALVES)]
+        early = []
+        for m, half in outputs[:EARLY_BANKS]:
+            bank = banks.tile([P, N_TILE], F32, tag="bank")
+            early.append((bank, m, half))
+        for g in range(last):
+            for bank, m, half in early:
+                down_pass(bank, m, half, g)
+        for bank, m, half in early:
+            down_pass(bank, m, half, last)
+            store(bank, m, half)
+        for m, half in outputs[EARLY_BANKS:]:
+            bank = banks.tile([P, N_TILE], F32, tag="bank")
+            for g in range(FF_CHUNKS):
+                down_pass(bank, m, half, g)
+            store(bank, m, half)

@@ -34,7 +34,9 @@ PLANES_PER_TILE = 4
 PIECE = 256
 TILES_PER_PIECE = PIECE // P
 PIECES = D_FF // PIECE
-PIECES_UP_FRONT = 4
+LOADS_UP_FRONT = 10
+
+CHUNK_GROUPS = ((0, 1), (2, 3), (4,))
 
 VECTOR_SHARE = 320
 EARLY_BANKS = 5
@@ -54,7 +56,7 @@ def tile_mixllamamlp_kernel(
         x_stage = ctx.enter_context(tc.tile_pool(name="x_stage", bufs=4))
         silu_pool = ctx.enter_context(tc.tile_pool(name="silu_pool", bufs=3))
         h_stage = ctx.enter_context(tc.tile_pool(name="h_stage", bufs=2))
-        y_pool = ctx.enter_context(tc.tile_pool(name="y_pool", bufs=4))
+        y_pool = ctx.enter_context(tc.tile_pool(name="y_pool", bufs=8))
         banks = ctx.enter_context(tc.psum_pool(name="banks", bufs=8))
         ctx.enter_context(tc.manual_schedule())
 
@@ -113,22 +115,23 @@ def tile_mixllamamlp_kernel(
             nc.sync.dma_start(out=pass_words[:], in_=W_down_words[g].rearrange("p n t -> p (n t)").bitcast(I32))
             down_words[g] = pass_words
 
-        for piece in range(PIECES_UP_FRONT):
-            load_gate_up_piece(piece, 0)
-            load_gate_up_piece(piece, 1)
+        later_loads = []
+        for group in CHUNK_GROUPS:
+            for part in range(PIECES // FF_CHUNKS):
+                for c in group:
+                    for w in range(2):
+                        later_loads.append((load_gate_up_piece, (PIECES // FF_CHUNKS * c + part, w)))
+        for quadrant in range(QUADRANTS):
+            later_loads.append((load_down_planes, (quadrant,)))
+        for g in range(FF_CHUNKS):
+            later_loads.append((load_down_words, (g,)))
 
-        def load_behind_tile(i):
-            later = 2 * (PIECES - PIECES_UP_FRONT)
-            if i < later:
-                load_gate_up_piece(PIECES_UP_FRONT + i // 2, i % 2)
-            elif i < later + 2:
-                load_down_planes(2 * (i - later))
-                load_down_planes(2 * (i - later) + 1)
-            elif i < later + 5:
-                load_down_words(i - later - 2)
-            elif i == FEATURE_TILES - 1:
-                load_down_words(3)
-                load_down_words(4)
+        def issue_loads(count):
+            for load, arguments in later_loads[:count]:
+                load(*arguments)
+            later_loads[:count] = []
+
+        issue_loads(LOADS_UP_FRONT)
 
         x_codes = resident.tile([P, X_PASSES, TOKENS], U32, align_bytes=64)
         x_scales = resident.tile([P, X_PASSES, TOKENS], U8, align_bytes=64)
@@ -174,7 +177,6 @@ def tile_mixllamamlp_kernel(
 
         h_codes = resident.tile([P, FF_CHUNKS, TOKENS], U32, align_bytes=64)
         h_scales = resident.tile([P, FF_CHUNKS, TOKENS], U8, align_bytes=64)
-        h_rows = {}
         h_sorted = {}
         h_grouped = {}
 
@@ -194,23 +196,17 @@ def tile_mixllamamlp_kernel(
                 )
             return bank
 
-        def feature_tile(c, j):
+        def feature_tile(c, j, rows):
             i = TILES_PER_CHUNK * c + j
             gate_bank = project(0, i)
             up_bank = project(1, i)
             silu_gate = silu_pool.tile([P, TOKENS], F32)
             nc.scalar.activation(out=silu_gate[:], in_=gate_bank[:], func=mybir.ActivationFunctionType.Silu)
-            nc.vector.tensor_tensor(
-                out=h_rows[c][:, j, :], in0=up_bank[:], in1=silu_gate[:], op=mybir.AluOpType.mult
-            )
-            for t in range(PACK):
-                nc.sync.dma_start(
-                    out=h_sorted[c][QUADRANT * j : QUADRANT * (j + 1), t, :], in_=h_rows[c][t:P:PACK, j, :]
-                )
+            nc.vector.tensor_tensor(out=rows, in0=up_bank[:], in1=silu_gate[:], op=mybir.AluOpType.mult)
 
         def group_h(c):
             grouped = h_stage.tile([P, TOKENS, PACK], BF16, align_bytes=64, name="h_grouped")
-            by_token = h_sorted[c][:].rearrange("p t r -> p r t")
+            by_token = h_sorted[c].rearrange("p t r -> p r t")
             nc.vector.tensor_copy(out=grouped[:, 0:VECTOR_SHARE, :], in_=by_token[:, 0:VECTOR_SHARE, :])
             nc.scalar.copy(out=grouped[:, VECTOR_SHARE:TOKENS, :], in_=by_token[:, VECTOR_SHARE:TOKENS, :])
             h_grouped[c] = grouped
@@ -222,19 +218,32 @@ def tile_mixllamamlp_kernel(
                 in_=h_grouped[c][:].rearrange("p r t -> p (r t)"),
             )
 
-        for c in range(FF_CHUNKS):
-            h_rows[c] = h_stage.tile([P, TILES_PER_CHUNK, TOKENS], BF16, name="h_rows")
-            h_sorted[c] = h_stage.tile([P, PACK, TOKENS], BF16, name="h_sorted")
+        waiting = []
+        tiles_done = 0
+        for group in CHUNK_GROUPS:
+            width = len(group)
+            h_rows = h_stage.tile([P, TILES_PER_CHUNK, width, TOKENS], BF16, name="h_rows")
+            h_sorted_group = h_stage.tile([P, width, PACK, TOKENS], BF16, name="h_sorted_group")
             for j in range(TILES_PER_CHUNK):
-                feature_tile(c, j)
-                load_behind_tile(TILES_PER_CHUNK * c + j)
-                if c > 0 and j == 2:
-                    group_h(c - 1)
-                if c > 0 and j == 3:
-                    quantise_h(c - 1)
+                for place, c in enumerate(group):
+                    feature_tile(c, j, h_rows[:, j, place, :])
+                    tiles_done += 1
+                    if waiting and waiting[0][0] <= tiles_done:
+                        due, work, chunk = waiting[0]
+                        waiting[:1] = []
+                        work(chunk)
+                for t in range(PACK):
+                    nc.sync.dma_start(
+                        out=h_sorted_group[QUADRANT * j : QUADRANT * (j + 1), :, t, :], in_=h_rows[t:P:PACK, j, :, :]
+                    )
+                issue_loads(width)
+            for place, c in enumerate(group):
+                h_sorted[c] = h_sorted_group[:, place, :, :]
+                waiting.append((tiles_done + 2, group_h, c))
+                waiting.append((tiles_done + 2, quantise_h, c))
+        for due, work, chunk in waiting:
+            work(chunk)
         last = FF_CHUNKS - 1
-        group_h(last)
-        quantise_h(last)
 
         def down_pass(bank, m, half, g):
             if g < PLANES_PER_TILE:

@@ -31,16 +31,6 @@ QUADRANT = 32
 PLANE_ROWS = 4
 PLANES_PER_TILE = 4
 
-PIECE = 256
-TILES_PER_PIECE = PIECE // P
-PIECES = D_FF // PIECE
-LOADS_UP_FRONT = 10
-
-CHUNK_GROUPS = ((0, 1), (2, 3), (4,))
-
-VECTOR_SHARE = 320
-EARLY_BANKS = 5
-
 FLOPS = 2 * TOKENS * D_MODEL * D_FF * 3
 
 
@@ -55,7 +45,7 @@ def tile_mixllamamlp_kernel(
         resident = ctx.enter_context(tc.tile_pool(name="resident", bufs=1))
         x_stage = ctx.enter_context(tc.tile_pool(name="x_stage", bufs=4))
         silu_pool = ctx.enter_context(tc.tile_pool(name="silu_pool", bufs=3))
-        h_stage = ctx.enter_context(tc.tile_pool(name="h_stage", bufs=2))
+        h_stage = ctx.enter_context(tc.tile_pool(name="h_stage", bufs=3))
         y_pool = ctx.enter_context(tc.tile_pool(name="y_pool", bufs=8))
         banks = ctx.enter_context(tc.psum_pool(name="banks", bufs=8))
         ctx.enter_context(tc.manual_schedule())
@@ -86,18 +76,17 @@ def tile_mixllamamlp_kernel(
                     in_=scales[:, PLANE_ROWS * quadrant : PLANE_ROWS * (quadrant + 1), :].bitcast(I32),
                 )
 
-        gate_up_words = {}
+        raw_words = {}
+        for c in range(FF_CHUNKS):
+            for w, words in enumerate((W_gate_words, W_up_words)):
+                raw = resident.tile([P, X_PASSES, K_PASS], I32, name="raw_words_%d_%d" % (c, w), align_bytes=64)
+                nc.sync.dma_start(
+                    out=raw[:],
+                    in_=words.rearrange("g p n t -> p g (n t)").bitcast(I32)[:, :, c * K_PASS : (c + 1) * K_PASS],
+                )
+                raw_words[c, w] = raw
 
-        def load_gate_up_piece(piece, w):
-            words = (W_gate_words, W_up_words)[w]
-            piece_words = resident.tile([P, X_PASSES, PIECE], I32, name="words_%d_%d" % (piece, w), align_bytes=64)
-            nc.sync.dma_start(
-                out=piece_words[:],
-                in_=words.rearrange("g p n t -> p g (n t)").bitcast(I32)[:, :, piece * PIECE : (piece + 1) * PIECE],
-            )
-            gate_up_words[piece, w] = piece_words
-
-        def load_down_planes(quadrant):
+        for quadrant in range(QUADRANTS):
             rows = slice(PLANE_ROWS * quadrant, PLANE_ROWS * (quadrant + 1))
             nc.sync.dma_start(
                 out=down_planes[QUADRANT * quadrant : QUADRANT * quadrant + PLANE_ROWS * PLANES_PER_TILE, 0, :].bitcast(I32),
@@ -108,30 +97,11 @@ def tile_mixllamamlp_kernel(
                 in_=W_down_scales[PLANES_PER_TILE, rows, :].bitcast(I32),
             )
 
-        down_words = {}
-
-        def load_down_words(g):
+        down_words = []
+        for g in range(FF_CHUNKS):
             pass_words = resident.tile([P, D_MODEL], I32, name="down_words_%d" % g, align_bytes=64)
             nc.sync.dma_start(out=pass_words[:], in_=W_down_words[g].rearrange("p n t -> p (n t)").bitcast(I32))
-            down_words[g] = pass_words
-
-        later_loads = []
-        for group in CHUNK_GROUPS:
-            for part in range(PIECES // FF_CHUNKS):
-                for c in group:
-                    for w in range(2):
-                        later_loads.append((load_gate_up_piece, (PIECES // FF_CHUNKS * c + part, w)))
-        for quadrant in range(QUADRANTS):
-            later_loads.append((load_down_planes, (quadrant,)))
-        for g in range(FF_CHUNKS):
-            later_loads.append((load_down_words, (g,)))
-
-        def issue_loads(count):
-            for load, arguments in later_loads[:count]:
-                load(*arguments)
-            later_loads[:count] = []
-
-        issue_loads(LOADS_UP_FRONT)
+            down_words.append(pass_words)
 
         x_codes = resident.tile([P, X_PASSES, TOKENS], U32, align_bytes=64)
         x_scales = resident.tile([P, X_PASSES, TOKENS], U8, align_bytes=64)
@@ -175,75 +145,94 @@ def tile_mixllamamlp_kernel(
                 quantise_x(m - 1)
         quantise_x(TOKEN_TILES - 1)
 
-        h_codes = resident.tile([P, FF_CHUNKS, TOKENS], U32, align_bytes=64)
-        h_scales = resident.tile([P, FF_CHUNKS, TOKENS], U8, align_bytes=64)
-        h_sorted = {}
-        h_grouped = {}
+        sorted_words = {}
+        sorted_planes = resident.tile([P, D_FF], U8, align_bytes=64)
 
-        def project(w, i):
-            bank = banks.tile([P, TOKENS], F32, tag="bank")
-            piece, place = divmod(i, TILES_PER_PIECE)
-            for g in range(X_PASSES):
-                plane_start = PLANE_ROWS * (X_PASSES * w + g)
-                nc.tensor.matmul_mx(
-                    out=bank[:],
-                    lhsT=gate_up_words[piece, w][:, g, place * P : (place + 1) * P].bitcast(FP8X4),
-                    lhsT_scale=gate_up_planes[plane_start:P, i * P : (i + 1) * P],
-                    rhs=x_codes[:, g, :].bitcast(FP8X4),
-                    rhs_scale=x_scales[:, g, :],
-                    start=(g == 0),
-                    stop=(g == X_PASSES - 1),
-                )
-            return bank
+        def sort_words(c, w):
+            in_order = resident.tile([P, X_PASSES, K_PASS], I32, name="sorted_words_%d_%d" % (c, w), align_bytes=64)
+            nc.vector.tensor_copy(
+                out=in_order[:].rearrange("p g (t m) -> p g m t", t=PACK),
+                in_=raw_words[c, w][:].rearrange("p g (m t) -> p g m t", t=PACK),
+            )
+            sorted_words[c, w] = in_order
 
-        def feature_tile(c, j, rows):
-            i = TILES_PER_CHUNK * c + j
-            gate_bank = project(0, i)
-            up_bank = project(1, i)
-            silu_gate = silu_pool.tile([P, TOKENS], F32)
-            nc.scalar.activation(out=silu_gate[:], in_=gate_bank[:], func=mybir.ActivationFunctionType.Silu)
-            nc.vector.tensor_tensor(out=rows, in0=up_bank[:], in1=silu_gate[:], op=mybir.AluOpType.mult)
-
-        def group_h(c):
-            grouped = h_stage.tile([P, TOKENS, PACK], BF16, align_bytes=64, name="h_grouped")
-            by_token = h_sorted[c].rearrange("p t r -> p r t")
-            nc.vector.tensor_copy(out=grouped[:, 0:VECTOR_SHARE, :], in_=by_token[:, 0:VECTOR_SHARE, :])
-            nc.scalar.copy(out=grouped[:, VECTOR_SHARE:TOKENS, :], in_=by_token[:, VECTOR_SHARE:TOKENS, :])
-            h_grouped[c] = grouped
-
-        def quantise_h(c):
-            nc.vector.quantize_mx(
-                out=h_codes[:, c, :].bitcast(FP8X4),
-                scales=h_scales[:, c, :],
-                in_=h_grouped[c][:].rearrange("p r t -> p (r t)"),
+        def sort_planes(c):
+            columns = slice(c * K_PASS, (c + 1) * K_PASS)
+            nc.vector.tensor_copy(
+                out=sorted_planes[:, columns].rearrange("p (t m) -> p m t", t=PACK),
+                in_=gate_up_planes[:, columns].rearrange("p (m t) -> p m t", t=PACK),
             )
 
-        waiting = []
-        tiles_done = 0
-        for group in CHUNK_GROUPS:
-            width = len(group)
-            h_rows = h_stage.tile([P, TILES_PER_CHUNK, width, TOKENS], BF16, name="h_rows")
-            h_sorted_group = h_stage.tile([P, width, PACK, TOKENS], BF16, name="h_sorted_group")
-            for j in range(TILES_PER_CHUNK):
-                for place, c in enumerate(group):
-                    feature_tile(c, j, h_rows[:, j, place, :])
-                    tiles_done += 1
-                    if waiting and waiting[0][0] <= tiles_done:
-                        due, work, chunk = waiting[0]
-                        waiting[:1] = []
-                        work(chunk)
-                for t in range(PACK):
-                    nc.sync.dma_start(
-                        out=h_sorted_group[QUADRANT * j : QUADRANT * (j + 1), :, t, :], in_=h_rows[t:P:PACK, j, :, :]
+        h_codes = resident.tile([P, FF_CHUNKS, TOKENS], U32, align_bytes=64)
+        h_scales = resident.tile([P, FF_CHUNKS, TOKENS], U8, align_bytes=64)
+        h_grouped = {}
+
+        def project(w, c, m):
+            bank = banks.tile([P, PACK, P], F32, tag="bank")
+            for t in range(PACK):
+                for g in range(X_PASSES):
+                    plane_start = PLANE_ROWS * (X_PASSES * w + g)
+                    nc.tensor.matmul_mx(
+                        out=bank[:, t, :],
+                        lhsT=sorted_words[c, w][:, g, t * P : (t + 1) * P].bitcast(FP8X4),
+                        lhsT_scale=sorted_planes[plane_start:P, c * K_PASS + t * P : c * K_PASS + (t + 1) * P],
+                        rhs=x_codes[:, g, m * P : (m + 1) * P].bitcast(FP8X4),
+                        rhs_scale=x_scales[:, g, m * P : (m + 1) * P],
+                        start=(g == 0),
+                        stop=(g == X_PASSES - 1),
                     )
-                issue_loads(width)
-            for place, c in enumerate(group):
-                h_sorted[c] = h_sorted_group[:, place, :, :]
-                waiting.append((tiles_done + 2, group_h, c))
-                waiting.append((tiles_done + 2, quantise_h, c))
-        for due, work, chunk in waiting:
-            work(chunk)
+            return bank
+
+        def gate_up_unit(c, m):
+            gate_bank = project(0, c, m)
+            up_bank = project(1, c, m)
+            silu_gate = silu_pool.tile([P, P, PACK], F32)
+            nc.scalar.activation(
+                out=silu_gate[:],
+                in_=gate_bank[:].rearrange("p t r -> p r t"),
+                func=mybir.ActivationFunctionType.Silu,
+            )
+            nc.vector.tensor_tensor(
+                out=h_grouped[c][:, m * P : (m + 1) * P, :],
+                in0=up_bank[:].rearrange("p t r -> p r t"),
+                in1=silu_gate[:],
+                op=mybir.AluOpType.mult,
+            )
+
+        def quantise_h(c, first, end):
+            nc.vector.quantize_mx(
+                out=h_codes[:, c, first:end].bitcast(FP8X4),
+                scales=h_scales[:, c, first:end],
+                in_=h_grouped[c][:, first:end, :].rearrange("p r t -> p (r t)"),
+            )
+
         last = FF_CHUNKS - 1
+        waiting = []
+        for c in range(1, FF_CHUNKS):
+            ahead = TOKEN_TILES * c - 5
+            waiting.append((max(ahead, 1), sort_words, (c, 0)))
+            waiting.append((max(ahead + 1, 1), sort_words, (c, 1)))
+            waiting.append((max(ahead + 2, 2), sort_planes, (c,)))
+        for c in range(last):
+            waiting.append((TOKEN_TILES * (c + 1) + 1, quantise_h, (c, 0, TOKENS)))
+        for m in range(TOKEN_TILES):
+            waiting.append((TOKEN_TILES * last + m + 2, quantise_h, (last, m * P, (m + 1) * P)))
+
+        sort_planes(0)
+        sort_words(0, 0)
+        sort_words(0, 1)
+        units_done = 0
+        for c in range(FF_CHUNKS):
+            h_grouped[c] = h_stage.tile([P, TOKENS, PACK], BF16, align_bytes=64, name="h_grouped")
+            for m in range(TOKEN_TILES):
+                gate_up_unit(c, m)
+                units_done += 1
+                for due, work, arguments in waiting:
+                    if due == units_done:
+                        work(*arguments)
+        for due, work, arguments in waiting:
+            if due > units_done:
+                work(*arguments)
 
         def down_pass(bank, m, half, g):
             if g < PLANES_PER_TILE:
@@ -268,19 +257,9 @@ def tile_mixllamamlp_kernel(
                 nc.scalar.copy(out=y_tile[:], in_=bank[:])
             nc.sync.dma_start(out=out_rows[m * P : (m + 1) * P, half * N_TILE : (half + 1) * N_TILE], in_=y_tile[:])
 
-        outputs = [(m, half) for m in range(TOKEN_TILES) for half in range(OUT_HALVES)]
-        early = []
-        for m, half in outputs[:EARLY_BANKS]:
-            bank = banks.tile([P, N_TILE], F32, tag="bank")
-            early.append((bank, m, half))
-        for g in range(last):
-            for bank, m, half in early:
-                down_pass(bank, m, half, g)
-        for bank, m, half in early:
-            down_pass(bank, m, half, last)
-            store(bank, m, half)
-        for m, half in outputs[EARLY_BANKS:]:
-            bank = banks.tile([P, N_TILE], F32, tag="bank")
-            for g in range(FF_CHUNKS):
-                down_pass(bank, m, half, g)
-            store(bank, m, half)
+        for m in range(TOKEN_TILES):
+            for half in range(OUT_HALVES):
+                bank = banks.tile([P, N_TILE], F32, tag="bank")
+                for g in range(FF_CHUNKS):
+                    down_pass(bank, m, half, g)
+                store(bank, m, half)

@@ -31,6 +31,8 @@ QUADRANT = 32
 PLANE_ROWS = 4
 PLANES_PER_TILE = 4
 
+WARM_UP_MATMULS = 6
+
 FLOPS = 2 * TOKENS * D_MODEL * D_FF * 3
 
 
@@ -144,6 +146,12 @@ def tile_mixllamamlp_kernel(
             if m > 0:
                 quantise_x(m - 1)
         quantise_x(TOKEN_TILES - 1)
+
+        warm_bank = banks.tile([P, N_TILE], F32, tag="bank")
+        for repeat in range(WARM_UP_MATMULS):
+            nc.tensor.matmul(
+                out=warm_bank[:], lhsT=x_tiles[0][:, 0:P], rhs=x_tiles[0][:, 0:N_TILE], start=True, stop=True
+            )
 
         sorted_words = {}
         sorted_planes = resident.tile([P, D_FF], U8, align_bytes=64)

@@ -33,6 +33,8 @@ PLANES_PER_TILE = 4
 
 WARM_UP_MATMULS = 6
 
+WIDE_CHUNKS = 3
+
 FLOPS = 2 * TOKENS * D_MODEL * D_FF * 3
 
 
@@ -207,6 +209,40 @@ def tile_mixllamamlp_kernel(
                 op=mybir.AluOpType.mult,
             )
 
+        h_sorted = {}
+
+        def project_wide(w, c, t):
+            bank = banks.tile([P, TOKENS], F32, tag="bank")
+            for g in range(X_PASSES):
+                plane_start = PLANE_ROWS * (X_PASSES * w + g)
+                nc.tensor.matmul_mx(
+                    out=bank[:],
+                    lhsT=sorted_words[c, w][:, g, t * P : (t + 1) * P].bitcast(FP8X4),
+                    lhsT_scale=sorted_planes[plane_start:P, c * K_PASS + t * P : c * K_PASS + (t + 1) * P],
+                    rhs=x_codes[:, g, :].bitcast(FP8X4),
+                    rhs_scale=x_scales[:, g, :],
+                    start=(g == 0),
+                    stop=(g == X_PASSES - 1),
+                )
+            return bank
+
+        def wide_unit(c, t):
+            gate_bank = project_wide(0, c, t)
+            up_bank = project_wide(1, c, t)
+            silu_gate = silu_pool.tile([P, TOKENS], F32)
+            nc.scalar.activation(out=silu_gate[:], in_=gate_bank[:], func=mybir.ActivationFunctionType.Silu)
+            nc.vector.tensor_tensor(
+                out=h_sorted[c][:, t, :], in0=up_bank[:], in1=silu_gate[:], op=mybir.AluOpType.mult
+            )
+
+        def group_h(c, m):
+            if m == 0:
+                h_grouped[c] = h_stage.tile([P, TOKENS, PACK], BF16, align_bytes=64, name="h_grouped")
+            nc.scalar.copy(
+                out=h_grouped[c][:, m * P : (m + 1) * P, :],
+                in_=h_sorted[c][:, :, m * P : (m + 1) * P].rearrange("p t r -> p r t"),
+            )
+
         def quantise_h(c, first, end):
             nc.vector.quantize_mx(
                 out=h_codes[:, c, first:end].bitcast(FP8X4),
@@ -222,7 +258,12 @@ def tile_mixllamamlp_kernel(
             waiting.append((max(ahead + 1, 1), sort_words, (c, 1)))
             waiting.append((max(ahead + 2, 2), sort_planes, (c,)))
         for c in range(last):
-            waiting.append((TOKEN_TILES * (c + 1) + 1, quantise_h, (c, 0, TOKENS)))
+            behind = TOKEN_TILES * (c + 1) + 1
+            if c < WIDE_CHUNKS:
+                for m in range(TOKEN_TILES):
+                    waiting.append((behind + m, group_h, (c, m)))
+                behind += TOKEN_TILES
+            waiting.append((behind, quantise_h, (c, 0, TOKENS)))
         for m in range(TOKEN_TILES):
             waiting.append((TOKEN_TILES * last + m + 2, quantise_h, (last, m * P, (m + 1) * P)))
 
@@ -231,9 +272,15 @@ def tile_mixllamamlp_kernel(
         sort_words(0, 1)
         units_done = 0
         for c in range(FF_CHUNKS):
-            h_grouped[c] = h_stage.tile([P, TOKENS, PACK], BF16, align_bytes=64, name="h_grouped")
+            if c < WIDE_CHUNKS:
+                h_sorted[c] = h_stage.tile([P, PACK, TOKENS], BF16, name="h_sorted")
+            else:
+                h_grouped[c] = h_stage.tile([P, TOKENS, PACK], BF16, align_bytes=64, name="h_grouped")
             for m in range(TOKEN_TILES):
-                gate_up_unit(c, m)
+                if c < WIDE_CHUNKS:
+                    wide_unit(c, m)
+                else:
+                    gate_up_unit(c, m)
                 units_done += 1
                 for due, work, arguments in waiting:
                     if due == units_done:

@@ -48,7 +48,7 @@ def tile_mixllamamlp_kernel(
     with ExitStack() as ctx:
         resident = ctx.enter_context(tc.tile_pool(name="resident", bufs=1))
         x_stage = ctx.enter_context(tc.tile_pool(name="x_stage", bufs=4))
-        silu_pool = ctx.enter_context(tc.tile_pool(name="silu_pool", bufs=3))
+        silu_pool = ctx.enter_context(tc.tile_pool(name="silu_pool", bufs=4))
         h_stage = ctx.enter_context(tc.tile_pool(name="h_stage", bufs=3))
         y_pool = ctx.enter_context(tc.tile_pool(name="y_pool", bufs=8))
         banks = ctx.enter_context(tc.psum_pool(name="banks", bufs=8))
@@ -72,6 +72,18 @@ def tile_mixllamamlp_kernel(
             nc.sync.dma_start(out=x_tile[:], in_=x_rows[m * P : (m + 1) * P, :])
             x_tiles.append(x_tile)
 
+        raw_words = {}
+
+        def load_raw_words(c, w):
+            words = (W_gate_words, W_up_words)[w]
+            raw = resident.tile([P, X_PASSES, K_PASS], I32, name="raw_words_%d_%d" % (c, w), align_bytes=64)
+            nc.sync.dma_start(
+                out=raw[:],
+                in_=words.rearrange("g p n t -> p g (n t)").bitcast(I32)[:, :, c * K_PASS : (c + 1) * K_PASS],
+            )
+            raw_words[c, w] = raw
+
+        load_raw_words(0, 0)
         for quadrant in range(QUADRANTS):
             for w, scales in enumerate((W_gate_scales, W_up_scales)):
                 first = QUADRANT * quadrant + PLANE_ROWS * X_PASSES * w
@@ -79,16 +91,10 @@ def tile_mixllamamlp_kernel(
                     out=gate_up_planes[first : first + PLANE_ROWS * X_PASSES, :].bitcast(I32),
                     in_=scales[:, PLANE_ROWS * quadrant : PLANE_ROWS * (quadrant + 1), :].bitcast(I32),
                 )
-
-        raw_words = {}
-        for c in range(FF_CHUNKS):
-            for w, words in enumerate((W_gate_words, W_up_words)):
-                raw = resident.tile([P, X_PASSES, K_PASS], I32, name="raw_words_%d_%d" % (c, w), align_bytes=64)
-                nc.sync.dma_start(
-                    out=raw[:],
-                    in_=words.rearrange("g p n t -> p g (n t)").bitcast(I32)[:, :, c * K_PASS : (c + 1) * K_PASS],
-                )
-                raw_words[c, w] = raw
+        load_raw_words(0, 1)
+        for c in range(1, FF_CHUNKS):
+            for w in range(2):
+                load_raw_words(c, w)
 
         for quadrant in range(QUADRANTS):
             rows = slice(PLANE_ROWS * quadrant, PLANE_ROWS * (quadrant + 1))
@@ -226,11 +232,14 @@ def tile_mixllamamlp_kernel(
                 )
             return bank
 
-        def wide_unit(c, t):
+        def wide_gate(c, t):
             gate_bank = project_wide(0, c, t)
-            up_bank = project_wide(1, c, t)
             silu_gate = silu_pool.tile([P, TOKENS], F32)
             nc.scalar.activation(out=silu_gate[:], in_=gate_bank[:], func=mybir.ActivationFunctionType.Silu)
+            return silu_gate
+
+        def wide_up(c, t, silu_gate):
+            up_bank = project_wide(1, c, t)
             nc.vector.tensor_tensor(
                 out=h_sorted[c][:, t, :], in0=up_bank[:], in1=silu_gate[:], op=mybir.AluOpType.mult
             )
@@ -254,9 +263,9 @@ def tile_mixllamamlp_kernel(
         waiting = []
         for c in range(1, FF_CHUNKS):
             ahead = TOKEN_TILES * c - 5
-            waiting.append((max(ahead, 1), sort_words, (c, 0)))
-            waiting.append((max(ahead + 1, 1), sort_words, (c, 1)))
-            waiting.append((max(ahead + 2, 2), sort_planes, (c,)))
+            waiting.append((max(ahead, 0), sort_planes, (c,)))
+            waiting.append((max(ahead + 1, 0), sort_words, (c, 0)))
+            waiting.append((max(ahead + 2, 1), sort_words, (c, 1)))
         for c in range(last):
             behind = TOKEN_TILES * (c + 1) + 1
             if c < WIDE_CHUNKS:
@@ -267,54 +276,62 @@ def tile_mixllamamlp_kernel(
         for m in range(TOKEN_TILES):
             waiting.append((TOKEN_TILES * last + m + 2, quantise_h, (last, m * P, (m + 1) * P)))
 
-        sort_planes(0)
+        def issue_waiting(units_done):
+            for due, work, arguments in waiting:
+                if due == units_done:
+                    work(*arguments)
+
         sort_words(0, 0)
+        sort_planes(0)
         sort_words(0, 1)
         units_done = 0
+        issue_waiting(units_done)
         for c in range(FF_CHUNKS):
             if c < WIDE_CHUNKS:
                 h_sorted[c] = h_stage.tile([P, PACK, TOKENS], BF16, name="h_sorted")
             else:
                 h_grouped[c] = h_stage.tile([P, TOKENS, PACK], BF16, align_bytes=64, name="h_grouped")
+            if c == 0:
+                ready = [wide_gate(c, t) for t in range(PACK)]
             for m in range(TOKEN_TILES):
-                if c < WIDE_CHUNKS:
-                    wide_unit(c, m)
+                if c == 0:
+                    wide_up(c, m, ready[m])
+                elif c < WIDE_CHUNKS:
+                    wide_up(c, m, wide_gate(c, m))
                 else:
                     gate_up_unit(c, m)
                 units_done += 1
-                for due, work, arguments in waiting:
-                    if due == units_done:
-                        work(*arguments)
+                issue_waiting(units_done)
         for due, work, arguments in waiting:
             if due > units_done:
                 work(*arguments)
 
-        def down_pass(bank, m, half, g):
+        def down_pass(bank, m, columns, g):
             if g < PLANES_PER_TILE:
-                plane = down_planes[PLANE_ROWS * g : P, 0, half * N_TILE : (half + 1) * N_TILE]
+                plane = down_planes[PLANE_ROWS * g : P, 0, columns]
             else:
-                plane = down_planes[:, 1, half * N_TILE : (half + 1) * N_TILE]
+                plane = down_planes[:, 1, columns]
             nc.tensor.matmul_mx(
                 out=bank[:],
                 lhsT=h_codes[:, g, m * P : (m + 1) * P].bitcast(FP8X4),
                 lhsT_scale=h_scales[:, g, m * P : (m + 1) * P],
-                rhs=down_words[g][:, half * N_TILE : (half + 1) * N_TILE].bitcast(FP8X4),
+                rhs=down_words[g][:, columns].bitcast(FP8X4),
                 rhs_scale=plane,
                 start=(g == 0),
                 stop=(g == FF_CHUNKS - 1),
             )
 
-        def store(bank, m, half):
-            y_tile = y_pool.tile([P, N_TILE], F32)
-            if half == 0:
+        pieces = [(m, half * N_TILE, N_TILE) for m in range(TOKEN_TILES) for half in range(OUT_HALVES)]
+        m, first, width = pieces[-1]
+        pieces[-1:] = [(m, first, width // 2), (m, first + width // 2, width // 2)]
+        for number, (m, first, width) in enumerate(pieces):
+            columns = slice(first, first + width)
+            bank = banks.tile([P, width], F32, tag="bank")
+            for g in range(FF_CHUNKS):
+                down_pass(bank, m, columns, g)
+            y_tile = y_pool.tile([P, width], F32)
+            if number % 2 == 0:
                 nc.vector.tensor_copy(out=y_tile[:], in_=bank[:])
             else:
                 nc.scalar.copy(out=y_tile[:], in_=bank[:])
-            nc.sync.dma_start(out=out_rows[m * P : (m + 1) * P, half * N_TILE : (half + 1) * N_TILE], in_=y_tile[:])
-
-        for m in range(TOKEN_TILES):
-            for half in range(OUT_HALVES):
-                bank = banks.tile([P, N_TILE], F32, tag="bank")
-                for g in range(FF_CHUNKS):
-                    down_pass(bank, m, half, g)
-                store(bank, m, half)
+            nc.sync.dma_start(out=out_rows[m * P : (m + 1) * P, columns], in_=y_tile[:])

@@ -31,9 +31,14 @@ QUADRANT = 32
 PLANE_ROWS = 4
 PLANES_PER_TILE = 4
 
-WARM_UP_MATMULS = 6
+WARM_UP_BEFORE_X = 4
+WARM_UP_BEHIND_X = 3
 
 WIDE_CHUNKS = 3
+
+FIRST_PLANES = 2
+
+FIRST_MOVING = 256
 
 FLOPS = 2 * TOKENS * D_MODEL * D_FF * 3
 
@@ -54,14 +59,22 @@ def tile_mixllamamlp_kernel(
         banks = ctx.enter_context(tc.psum_pool(name="banks", bufs=8))
         ctx.enter_context(tc.manual_schedule())
 
-        gate_up_planes = resident.tile([P, D_FF], U8, align_bytes=64)
-        down_planes = resident.tile([P, 2, D_MODEL], U8, align_bytes=64)
-        nc.vector.memset(gate_up_planes[:].bitcast(I32), 0)
-        nc.vector.memset(down_planes[:].rearrange("p s n -> p (s n)").bitcast(I32), 0)
-
+        zeros = resident.tile([P, N_TILE], BF16, align_bytes=64)
+        nc.vector.memset(zeros[:].bitcast(I32), 0)
         table_warmer = resident.tile([P, 1], F32)
         nc.vector.memset(table_warmer[:], 0.0)
         nc.scalar.activation(out=table_warmer[:], in_=table_warmer[:], func=mybir.ActivationFunctionType.Silu)
+
+        early = FIRST_PLANES * K_PASS
+        first_planes = []
+        for w in range(2):
+            planes = resident.tile([P, early], U8, name="first_planes_%d" % w, align_bytes=64)
+            nc.vector.memset(planes[:].bitcast(I32), 0)
+            first_planes.append(planes)
+        gate_up_planes = resident.tile([P, D_FF - early], U8, align_bytes=64)
+        down_planes = resident.tile([P, 2, D_MODEL], U8, align_bytes=64)
+        nc.vector.memset(gate_up_planes[:].bitcast(I32), 0)
+        nc.vector.memset(down_planes[:].rearrange("p s n -> p (s n)").bitcast(I32), 0)
 
         identity_f32 = resident.tile([P, P], F32)
         make_identity(nc, identity_f32[:])
@@ -74,27 +87,40 @@ def tile_mixllamamlp_kernel(
 
         raw_words = {}
 
-        def load_raw_words(c, w):
+        def load_raw_words(c, w, first_pass, end_pass):
             words = (W_gate_words, W_up_words)[w]
-            raw = resident.tile([P, X_PASSES, K_PASS], I32, name="raw_words_%d_%d" % (c, w), align_bytes=64)
+            if first_pass == 0:
+                raw_words[c, w] = resident.tile(
+                    [P, X_PASSES, K_PASS], I32, name="raw_words_%d_%d" % (c, w), align_bytes=64
+                )
             nc.sync.dma_start(
-                out=raw[:],
-                in_=words.rearrange("g p n t -> p g (n t)").bitcast(I32)[:, :, c * K_PASS : (c + 1) * K_PASS],
+                out=raw_words[c, w][:, first_pass:end_pass, :],
+                in_=words.rearrange("g p n t -> p g (n t)").bitcast(I32)[
+                    :, first_pass:end_pass, c * K_PASS : (c + 1) * K_PASS
+                ],
             )
-            raw_words[c, w] = raw
 
-        load_raw_words(0, 0)
-        for quadrant in range(QUADRANTS):
-            for w, scales in enumerate((W_gate_scales, W_up_scales)):
+        def load_planes(planes, w, columns):
+            scales = (W_gate_scales, W_up_scales)[w]
+            for quadrant in range(QUADRANTS):
                 first = QUADRANT * quadrant + PLANE_ROWS * X_PASSES * w
                 nc.sync.dma_start(
-                    out=gate_up_planes[first : first + PLANE_ROWS * X_PASSES, :].bitcast(I32),
-                    in_=scales[:, PLANE_ROWS * quadrant : PLANE_ROWS * (quadrant + 1), :].bitcast(I32),
+                    out=planes[first : first + PLANE_ROWS * X_PASSES, :].bitcast(I32),
+                    in_=scales[:, PLANE_ROWS * quadrant : PLANE_ROWS * (quadrant + 1), columns].bitcast(I32),
                 )
-        load_raw_words(0, 1)
-        for c in range(1, FF_CHUNKS):
+
+        load_planes(first_planes[0], 0, slice(0, early))
+        load_raw_words(0, 0, 0, 1)
+        load_raw_words(0, 0, 1, 2)
+        load_planes(first_planes[1], 1, slice(0, early))
+        load_raw_words(0, 1, 0, 2)
+        load_raw_words(1, 0, 0, 2)
+        load_raw_words(1, 1, 0, 2)
+        for w in range(2):
+            load_planes(gate_up_planes, w, slice(early, D_FF))
+        for c in range(2, FF_CHUNKS):
             for w in range(2):
-                load_raw_words(c, w)
+                load_raw_words(c, w, 0, 2)
 
         for quadrant in range(QUADRANTS):
             rows = slice(PLANE_ROWS * quadrant, PLANE_ROWS * (quadrant + 1))
@@ -135,10 +161,7 @@ def tile_mixllamamlp_kernel(
                 .rearrange("p (g r u) -> p g r u", g=X_PASSES, u=2)
             )
             transposed = bank[:].rearrange("p (g u) r -> p g r u", u=2)
-            if m % 2 == 0:
-                nc.vector.tensor_copy(out=grouped_words, in_=transposed)
-            else:
-                nc.scalar.copy(out=grouped_words, in_=transposed)
+            nc.scalar.copy(out=grouped_words, in_=transposed)
             x_grouped[m] = grouped
 
         def quantise_x(m):
@@ -149,35 +172,59 @@ def tile_mixllamamlp_kernel(
                     in_=x_grouped[m][:, g, :, :].rearrange("p r t -> p (r t)"),
                 )
 
+        warm_bank = banks.tile([P, N_TILE], F32, tag="bank")
+
+        def warm_up(matmuls):
+            for repeat in range(matmuls):
+                nc.tensor.matmul(out=warm_bank[:], lhsT=zeros[:, 0:P], rhs=zeros[:], start=True, stop=True)
+
+        warm_up(WARM_UP_BEFORE_X)
         for m in range(TOKEN_TILES):
             transpose_x(m)
+            warm_up(1)
             if m > 0:
                 quantise_x(m - 1)
-        quantise_x(TOKEN_TILES - 1)
-
-        warm_bank = banks.tile([P, N_TILE], F32, tag="bank")
-        for repeat in range(WARM_UP_MATMULS):
-            nc.tensor.matmul(
-                out=warm_bank[:], lhsT=x_tiles[0][:, 0:P], rhs=x_tiles[0][:, 0:N_TILE], start=True, stop=True
-            )
+        warm_up(WARM_UP_BEHIND_X)
 
         sorted_words = {}
-        sorted_planes = resident.tile([P, D_FF], U8, align_bytes=64)
+        first_sorted_planes = []
+        for w in range(2):
+            planes = resident.tile([P, early], U8, name="first_sorted_planes_%d" % w, align_bytes=64)
+            first_sorted_planes.append(planes)
+        sorted_planes = resident.tile([P, D_FF - early], U8, align_bytes=64)
 
-        def sort_words(c, w):
-            in_order = resident.tile([P, X_PASSES, K_PASS], I32, name="sorted_words_%d_%d" % (c, w), align_bytes=64)
+        def sort_words(c, w, first_pass, end_pass):
+            if first_pass == 0:
+                sorted_words[c, w] = resident.tile(
+                    [P, X_PASSES, K_PASS], I32, name="sorted_words_%d_%d" % (c, w), align_bytes=64
+                )
             nc.vector.tensor_copy(
-                out=in_order[:].rearrange("p g (t m) -> p g m t", t=PACK),
-                in_=raw_words[c, w][:].rearrange("p g (m t) -> p g m t", t=PACK),
+                out=sorted_words[c, w][:, first_pass:end_pass, :].rearrange("p g (t m) -> p g m t", t=PACK),
+                in_=raw_words[c, w][:, first_pass:end_pass, :].rearrange("p g (m t) -> p g m t", t=PACK),
             )
-            sorted_words[c, w] = in_order
+
+        def sort_plane_bytes(in_order, as_loaded):
+            nc.vector.tensor_copy(
+                out=in_order.rearrange("p (t m) -> p m t", t=PACK),
+                in_=as_loaded.rearrange("p (m t) -> p m t", t=PACK),
+            )
+
+        def sort_first_planes(c, w):
+            columns = slice(c * K_PASS, (c + 1) * K_PASS)
+            sort_plane_bytes(first_sorted_planes[w][:, columns], first_planes[w][:, columns])
 
         def sort_planes(c):
-            columns = slice(c * K_PASS, (c + 1) * K_PASS)
-            nc.vector.tensor_copy(
-                out=sorted_planes[:, columns].rearrange("p (t m) -> p m t", t=PACK),
-                in_=gate_up_planes[:, columns].rearrange("p (m t) -> p m t", t=PACK),
-            )
+            columns = slice((c - FIRST_PLANES) * K_PASS, (c - FIRST_PLANES + 1) * K_PASS)
+            sort_plane_bytes(sorted_planes[:, columns], gate_up_planes[:, columns])
+
+        def stationary(w, c, g, t):
+            plane_start = PLANE_ROWS * (X_PASSES * w + g)
+            first = c * K_PASS + t * P
+            if c < FIRST_PLANES:
+                plane = first_sorted_planes[w][plane_start:P, first : first + P]
+            else:
+                plane = sorted_planes[plane_start:P, first - early : first - early + P]
+            return sorted_words[c, w][:, g, t * P : (t + 1) * P].bitcast(FP8X4), plane
 
         h_codes = resident.tile([P, FF_CHUNKS, TOKENS], U32, align_bytes=64)
         h_scales = resident.tile([P, FF_CHUNKS, TOKENS], U8, align_bytes=64)
@@ -187,11 +234,11 @@ def tile_mixllamamlp_kernel(
             bank = banks.tile([P, PACK, P], F32, tag="bank")
             for t in range(PACK):
                 for g in range(X_PASSES):
-                    plane_start = PLANE_ROWS * (X_PASSES * w + g)
+                    codes, plane = stationary(w, c, g, t)
                     nc.tensor.matmul_mx(
                         out=bank[:, t, :],
-                        lhsT=sorted_words[c, w][:, g, t * P : (t + 1) * P].bitcast(FP8X4),
-                        lhsT_scale=sorted_planes[plane_start:P, c * K_PASS + t * P : c * K_PASS + (t + 1) * P],
+                        lhsT=codes,
+                        lhsT_scale=plane,
                         rhs=x_codes[:, g, m * P : (m + 1) * P].bitcast(FP8X4),
                         rhs_scale=x_scales[:, g, m * P : (m + 1) * P],
                         start=(g == 0),
@@ -220,11 +267,11 @@ def tile_mixllamamlp_kernel(
         def project_wide(w, c, t):
             bank = banks.tile([P, TOKENS], F32, tag="bank")
             for g in range(X_PASSES):
-                plane_start = PLANE_ROWS * (X_PASSES * w + g)
+                codes, plane = stationary(w, c, g, t)
                 nc.tensor.matmul_mx(
                     out=bank[:],
-                    lhsT=sorted_words[c, w][:, g, t * P : (t + 1) * P].bitcast(FP8X4),
-                    lhsT_scale=sorted_planes[plane_start:P, c * K_PASS + t * P : c * K_PASS + (t + 1) * P],
+                    lhsT=codes,
+                    lhsT_scale=plane,
                     rhs=x_codes[:, g, :].bitcast(FP8X4),
                     rhs_scale=x_scales[:, g, :],
                     start=(g == 0),
@@ -232,11 +279,34 @@ def tile_mixllamamlp_kernel(
                 )
             return bank
 
-        def wide_gate(c, t):
-            gate_bank = project_wide(0, c, t)
+        def silu_of(gate_bank):
             silu_gate = silu_pool.tile([P, TOKENS], F32)
             nc.scalar.activation(out=silu_gate[:], in_=gate_bank[:], func=mybir.ActivationFunctionType.Silu)
             return silu_gate
+
+        def wide_gate(c, t):
+            return silu_of(project_wide(0, c, t))
+
+        def first_gates():
+            gate_banks = []
+            for t in range(PACK):
+                gate_bank = banks.tile([P, TOKENS], F32, tag="bank", name="gate_bank")
+                gate_banks.append(gate_bank)
+            for first in range(0, TOKENS, FIRST_MOVING):
+                tokens = slice(first, first + FIRST_MOVING)
+                for g in range(X_PASSES):
+                    for t in range(PACK):
+                        codes, plane = stationary(0, 0, g, t)
+                        nc.tensor.matmul_mx(
+                            out=gate_banks[t][:, tokens],
+                            lhsT=codes,
+                            lhsT_scale=plane,
+                            rhs=x_codes[:, g, tokens].bitcast(FP8X4),
+                            rhs_scale=x_scales[:, g, tokens],
+                            start=(g == 0),
+                            stop=(g == X_PASSES - 1),
+                        )
+            return [silu_of(gate_bank) for gate_bank in gate_banks]
 
         def wide_up(c, t, silu_gate):
             up_bank = project_wide(1, c, t)
@@ -263,9 +333,14 @@ def tile_mixllamamlp_kernel(
         waiting = []
         for c in range(1, FF_CHUNKS):
             ahead = TOKEN_TILES * c - 5
-            waiting.append((max(ahead, 0), sort_planes, (c,)))
-            waiting.append((max(ahead + 1, 0), sort_words, (c, 0)))
-            waiting.append((max(ahead + 2, 1), sort_words, (c, 1)))
+            if c < FIRST_PLANES:
+                for w in range(2):
+                    waiting.append((w, sort_first_planes, (c, w)))
+                    waiting.append((w, sort_words, (c, w, 0, X_PASSES)))
+            else:
+                waiting.append((ahead, sort_planes, (c,)))
+                waiting.append((ahead + 1, sort_words, (c, 0, 0, X_PASSES)))
+                waiting.append((ahead + 2, sort_words, (c, 1, 0, X_PASSES)))
         for c in range(last):
             behind = TOKEN_TILES * (c + 1) + 1
             if c < WIDE_CHUNKS:
@@ -281,9 +356,12 @@ def tile_mixllamamlp_kernel(
                 if due == units_done:
                     work(*arguments)
 
-        sort_words(0, 0)
-        sort_planes(0)
-        sort_words(0, 1)
+        sort_first_planes(0, 0)
+        sort_words(0, 0, 0, 1)
+        quantise_x(TOKEN_TILES - 1)
+        sort_words(0, 0, 1, 2)
+        sort_first_planes(0, 1)
+        sort_words(0, 1, 0, X_PASSES)
         units_done = 0
         issue_waiting(units_done)
         for c in range(FF_CHUNKS):
@@ -292,7 +370,7 @@ def tile_mixllamamlp_kernel(
             else:
                 h_grouped[c] = h_stage.tile([P, TOKENS, PACK], BF16, align_bytes=64, name="h_grouped")
             if c == 0:
-                ready = [wide_gate(c, t) for t in range(PACK)]
+                ready = first_gates()
             for m in range(TOKEN_TILES):
                 if c == 0:
                     wide_up(c, m, ready[m])

@@ -34,7 +34,7 @@ PLANES_PER_TILE = 4
 WARM_UP_BEFORE_X = 4
 WARM_UP_BEHIND_X = 3
 
-WIDE_CHUNKS = 3
+OPEN_TILES = 2
 
 FIRST_PLANES = 2
 
@@ -230,38 +230,6 @@ def tile_mixllamamlp_kernel(
         h_scales = resident.tile([P, FF_CHUNKS, TOKENS], U8, align_bytes=64)
         h_grouped = {}
 
-        def project(w, c, m):
-            bank = banks.tile([P, PACK, P], F32, tag="bank")
-            for t in range(PACK):
-                for g in range(X_PASSES):
-                    codes, plane = stationary(w, c, g, t)
-                    nc.tensor.matmul_mx(
-                        out=bank[:, t, :],
-                        lhsT=codes,
-                        lhsT_scale=plane,
-                        rhs=x_codes[:, g, m * P : (m + 1) * P].bitcast(FP8X4),
-                        rhs_scale=x_scales[:, g, m * P : (m + 1) * P],
-                        start=(g == 0),
-                        stop=(g == X_PASSES - 1),
-                    )
-            return bank
-
-        def gate_up_unit(c, m):
-            gate_bank = project(0, c, m)
-            up_bank = project(1, c, m)
-            silu_gate = silu_pool.tile([P, P, PACK], F32)
-            nc.scalar.activation(
-                out=silu_gate[:],
-                in_=gate_bank[:].rearrange("p t r -> p r t"),
-                func=mybir.ActivationFunctionType.Silu,
-            )
-            nc.vector.tensor_tensor(
-                out=h_grouped[c][:, m * P : (m + 1) * P, :],
-                in0=up_bank[:].rearrange("p t r -> p r t"),
-                in1=silu_gate[:],
-                op=mybir.AluOpType.mult,
-            )
-
         h_sorted = {}
 
         def project_wide(w, c, t):
@@ -314,10 +282,10 @@ def tile_mixllamamlp_kernel(
                 out=h_sorted[c][:, t, :], in0=up_bank[:], in1=silu_gate[:], op=mybir.AluOpType.mult
             )
 
-        def group_h(c, m):
+        def group_h(c, m, copy):
             if m == 0:
                 h_grouped[c] = h_stage.tile([P, TOKENS, PACK], BF16, align_bytes=64, name="h_grouped")
-            nc.scalar.copy(
+            copy(
                 out=h_grouped[c][:, m * P : (m + 1) * P, :],
                 in_=h_sorted[c][:, :, m * P : (m + 1) * P].rearrange("p t r -> p r t"),
             )
@@ -343,13 +311,10 @@ def tile_mixllamamlp_kernel(
                 waiting.append((ahead + 2, sort_words, (c, 1, 0, X_PASSES)))
         for c in range(last):
             behind = TOKEN_TILES * (c + 1) + 1
-            if c < WIDE_CHUNKS:
-                for m in range(TOKEN_TILES):
-                    waiting.append((behind + m, group_h, (c, m)))
-                behind += TOKEN_TILES
-            waiting.append((behind, quantise_h, (c, 0, TOKENS)))
-        for m in range(TOKEN_TILES):
-            waiting.append((TOKEN_TILES * last + m + 2, quantise_h, (last, m * P, (m + 1) * P)))
+            for m in range(TOKEN_TILES):
+                waiting.append((behind + m, group_h, (c, m, nc.scalar.copy)))
+            if c + 1 < last:
+                waiting.append((behind + TOKEN_TILES, quantise_h, (c, 0, TOKENS)))
 
         def issue_waiting(units_done):
             for due, work, arguments in waiting:
@@ -365,24 +330,24 @@ def tile_mixllamamlp_kernel(
         units_done = 0
         issue_waiting(units_done)
         for c in range(FF_CHUNKS):
-            if c < WIDE_CHUNKS:
-                h_sorted[c] = h_stage.tile([P, PACK, TOKENS], BF16, name="h_sorted")
-            else:
-                h_grouped[c] = h_stage.tile([P, TOKENS, PACK], BF16, align_bytes=64, name="h_grouped")
+            h_sorted[c] = h_stage.tile([P, PACK, TOKENS], BF16, name="h_sorted")
             if c == 0:
                 ready = first_gates()
             for m in range(TOKEN_TILES):
                 if c == 0:
                     wide_up(c, m, ready[m])
-                elif c < WIDE_CHUNKS:
-                    wide_up(c, m, wide_gate(c, m))
                 else:
-                    gate_up_unit(c, m)
+                    wide_up(c, m, wide_gate(c, m))
                 units_done += 1
                 issue_waiting(units_done)
-        for due, work, arguments in waiting:
-            if due > units_done:
-                work(*arguments)
+
+        group_h(last, 0, nc.vector.tensor_copy)
+        group_h(last, 1, nc.vector.tensor_copy)
+        quantise_h(last - 1, 0, TOKENS)
+        for m in range(TOKEN_TILES):
+            quantise_h(last, m * P, (m + 1) * P)
+            if m + 2 < TOKEN_TILES:
+                group_h(last, m + 2, nc.vector.tensor_copy)
 
         def down_pass(bank, m, columns, g):
             if g < PLANES_PER_TILE:
@@ -399,17 +364,31 @@ def tile_mixllamamlp_kernel(
                 stop=(g == FF_CHUNKS - 1),
             )
 
-        pieces = [(m, half * N_TILE, N_TILE) for m in range(TOKEN_TILES) for half in range(OUT_HALVES)]
-        m, first, width = pieces[-1]
-        pieces[-1:] = [(m, first, width // 2), (m, first + width // 2, width // 2)]
-        for number, (m, first, width) in enumerate(pieces):
-            columns = slice(first, first + width)
-            bank = banks.tile([P, width], F32, tag="bank")
-            for g in range(FF_CHUNKS):
-                down_pass(bank, m, columns, g)
-            y_tile = y_pool.tile([P, width], F32)
+        def store_bank(number, bank, m, columns):
+            y_tile = y_pool.tile([P, columns.stop - columns.start], F32, name="y_tile")
             if number % 2 == 0:
                 nc.vector.tensor_copy(out=y_tile[:], in_=bank[:])
             else:
                 nc.scalar.copy(out=y_tile[:], in_=bank[:])
             nc.sync.dma_start(out=out_rows[m * P : (m + 1) * P, columns], in_=y_tile[:])
+
+        pieces = [(m, half * N_TILE, N_TILE) for m in range(TOKEN_TILES) for half in range(OUT_HALVES)]
+        m, first, width = pieces[-1]
+        pieces[-1:] = [(m, first, width // 2), (m, first + width // 2, width // 2)]
+        together = OPEN_TILES * OUT_HALVES
+        open_banks = []
+        for m, first, width in pieces[:together]:
+            bank = banks.tile([P, width], F32, tag="bank", name="open_bank")
+            open_banks.append(bank)
+        for g in range(FF_CHUNKS):
+            for bank, (m, first, width) in zip(open_banks, pieces):
+                down_pass(bank, m, slice(first, first + width), g)
+        for number, (m, first, width) in enumerate(pieces):
+            columns = slice(first, first + width)
+            if number < together:
+                bank = open_banks[number]
+            else:
+                bank = banks.tile([P, width], F32, tag="bank", name="bank")
+                for g in range(FF_CHUNKS):
+                    down_pass(bank, m, columns, g)
+            store_bank(number, bank, m, columns)

@@ -54,7 +54,7 @@ def tile_mixllamamlp_kernel(
         resident = ctx.enter_context(tc.tile_pool(name="resident", bufs=1))
         x_stage = ctx.enter_context(tc.tile_pool(name="x_stage", bufs=4))
         silu_pool = ctx.enter_context(tc.tile_pool(name="silu_pool", bufs=4))
-        h_stage = ctx.enter_context(tc.tile_pool(name="h_stage", bufs=3))
+        h_stage = ctx.enter_context(tc.tile_pool(name="h_stage", bufs=5))
         y_pool = ctx.enter_context(tc.tile_pool(name="y_pool", bufs=8))
         banks = ctx.enter_context(tc.psum_pool(name="banks", bufs=8))
         ctx.enter_context(tc.manual_schedule())
@@ -118,26 +118,9 @@ def tile_mixllamamlp_kernel(
         load_raw_words(1, 1, 0, 2)
         for w in range(2):
             load_planes(gate_up_planes, w, slice(early, D_FF))
-        for c in range(2, FF_CHUNKS):
+        for c in range(2, 4):
             for w in range(2):
                 load_raw_words(c, w, 0, 2)
-
-        for quadrant in range(QUADRANTS):
-            rows = slice(PLANE_ROWS * quadrant, PLANE_ROWS * (quadrant + 1))
-            nc.sync.dma_start(
-                out=down_planes[QUADRANT * quadrant : QUADRANT * quadrant + PLANE_ROWS * PLANES_PER_TILE, 0, :].bitcast(I32),
-                in_=W_down_scales[0:PLANES_PER_TILE, rows, :].bitcast(I32),
-            )
-            nc.sync.dma_start(
-                out=down_planes[QUADRANT * quadrant : QUADRANT * quadrant + PLANE_ROWS, 1, :].bitcast(I32),
-                in_=W_down_scales[PLANES_PER_TILE, rows, :].bitcast(I32),
-            )
-
-        down_words = []
-        for g in range(FF_CHUNKS):
-            pass_words = resident.tile([P, D_MODEL], I32, name="down_words_%d" % g, align_bytes=64)
-            nc.sync.dma_start(out=pass_words[:], in_=W_down_words[g].rearrange("p n t -> p (n t)").bitcast(I32))
-            down_words.append(pass_words)
 
         x_codes = resident.tile([P, X_PASSES, TOKENS], U32, align_bytes=64)
         x_scales = resident.tile([P, X_PASSES, TOKENS], U8, align_bytes=64)
@@ -184,24 +167,23 @@ def tile_mixllamamlp_kernel(
             warm_up(1)
             if m > 0:
                 quantise_x(m - 1)
+        quantise_x(TOKEN_TILES - 1)
         warm_up(WARM_UP_BEHIND_X)
 
         sorted_words = {}
         first_sorted_planes = []
         for w in range(2):
-            planes = resident.tile([P, early], U8, name="first_sorted_planes_%d" % w, align_bytes=64)
+            planes = resident.tile([P, early - K_PASS], U8, name="first_sorted_planes_%d" % w, align_bytes=64)
             first_sorted_planes.append(planes)
         sorted_planes = resident.tile([P, D_FF - early], U8, align_bytes=64)
 
-        def sort_words(c, w, first_pass, end_pass):
-            if first_pass == 0:
-                sorted_words[c, w] = resident.tile(
-                    [P, X_PASSES, K_PASS], I32, name="sorted_words_%d_%d" % (c, w), align_bytes=64
-                )
+        def sort_words(c, w):
+            in_order = resident.tile([P, X_PASSES, K_PASS], I32, name="sorted_words_%d_%d" % (c, w), align_bytes=64)
             nc.vector.tensor_copy(
-                out=sorted_words[c, w][:, first_pass:end_pass, :].rearrange("p g (t m) -> p g m t", t=PACK),
-                in_=raw_words[c, w][:, first_pass:end_pass, :].rearrange("p g (m t) -> p g m t", t=PACK),
+                out=in_order[:].rearrange("p g (t m) -> p g m t", t=PACK),
+                in_=raw_words[c, w][:].rearrange("p g (m t) -> p g m t", t=PACK),
             )
+            sorted_words[c, w] = in_order
 
         def sort_plane_bytes(in_order, as_loaded):
             nc.vector.tensor_copy(
@@ -211,7 +193,7 @@ def tile_mixllamamlp_kernel(
 
         def sort_first_planes(c, w):
             columns = slice(c * K_PASS, (c + 1) * K_PASS)
-            sort_plane_bytes(first_sorted_planes[w][:, columns], first_planes[w][:, columns])
+            sort_plane_bytes(first_sorted_planes[w][:], first_planes[w][:, columns])
 
         def sort_planes(c):
             columns = slice((c - FIRST_PLANES) * K_PASS, (c - FIRST_PLANES + 1) * K_PASS)
@@ -220,17 +202,51 @@ def tile_mixllamamlp_kernel(
         def stationary(w, c, g, t):
             plane_start = PLANE_ROWS * (X_PASSES * w + g)
             first = c * K_PASS + t * P
-            if c < FIRST_PLANES:
-                plane = first_sorted_planes[w][plane_start:P, first : first + P]
+            words = raw_words[c, w] if c == 0 else sorted_words[c, w]
+            if c == 0:
+                plane = first_planes[w][plane_start:P, first : first + P]
+            elif c < FIRST_PLANES:
+                plane = first_sorted_planes[w][plane_start:P, first - K_PASS : first - K_PASS + P]
             else:
                 plane = sorted_planes[plane_start:P, first - early : first - early + P]
-            return sorted_words[c, w][:, g, t * P : (t + 1) * P].bitcast(FP8X4), plane
+            return words[:, g, t * P : (t + 1) * P].bitcast(FP8X4), plane
 
         h_codes = resident.tile([P, FF_CHUNKS, TOKENS], U32, align_bytes=64)
         h_scales = resident.tile([P, FF_CHUNKS, TOKENS], U8, align_bytes=64)
         h_grouped = {}
 
+        last = FF_CHUNKS - 1
         h_sorted = {}
+        h_natural = resident.tile([P, TILES_PER_CHUNK, TOKENS], BF16)
+
+        def move_rows():
+            for j in range(TILES_PER_CHUNK):
+                for t in range(PACK):
+                    nc.sync.dma_start(
+                        out=h_sorted[0][QUADRANT * j : QUADRANT * (j + 1), t, :], in_=h_natural[t:P:PACK, j, :]
+                    )
+
+        down_order = [1, 2, 0, 3, 4]
+        down_words = {}
+
+        def load_the_rest():
+            for w in range(2):
+                load_raw_words(last, w, 0, 2)
+            for quadrant in range(QUADRANTS):
+                rows = slice(PLANE_ROWS * quadrant, PLANE_ROWS * (quadrant + 1))
+                nc.sync.dma_start(
+                    out=down_planes[QUADRANT * quadrant : QUADRANT * quadrant + PLANE_ROWS * PLANES_PER_TILE, 0, :].bitcast(I32),
+                    in_=W_down_scales[0:PLANES_PER_TILE, rows, :].bitcast(I32),
+                )
+                nc.sync.dma_start(
+                    out=down_planes[QUADRANT * quadrant : QUADRANT * quadrant + PLANE_ROWS, 1, :].bitcast(I32),
+                    in_=W_down_scales[PLANES_PER_TILE, rows, :].bitcast(I32),
+                )
+
+            for g in down_order:
+                pass_words = resident.tile([P, D_MODEL], I32, name="down_words_%d" % g, align_bytes=64)
+                nc.sync.dma_start(out=pass_words[:], in_=W_down_words[g].rearrange("p n t -> p (n t)").bitcast(I32))
+                down_words[g] = pass_words
 
         def project_wide(w, c, t):
             bank = banks.tile([P, TOKENS], F32, tag="bank")
@@ -278,8 +294,9 @@ def tile_mixllamamlp_kernel(
 
         def wide_up(c, t, silu_gate):
             up_bank = project_wide(1, c, t)
+            h_tile = h_natural if c == 0 else h_sorted[c]
             nc.vector.tensor_tensor(
-                out=h_sorted[c][:, t, :], in0=up_bank[:], in1=silu_gate[:], op=mybir.AluOpType.mult
+                out=h_tile[:, t, :], in0=up_bank[:], in1=silu_gate[:], op=mybir.AluOpType.mult
             )
 
         def group_h(c, m, copy):
@@ -297,36 +314,35 @@ def tile_mixllamamlp_kernel(
                 in_=h_grouped[c][:, first:end, :].rearrange("p r t -> p (r t)"),
             )
 
-        last = FF_CHUNKS - 1
         waiting = []
         for c in range(1, FF_CHUNKS):
             ahead = TOKEN_TILES * c - 5
             if c < FIRST_PLANES:
                 for w in range(2):
                     waiting.append((w, sort_first_planes, (c, w)))
-                    waiting.append((w, sort_words, (c, w, 0, X_PASSES)))
+                    waiting.append((w, sort_words, (c, w)))
             else:
                 waiting.append((ahead, sort_planes, (c,)))
-                waiting.append((ahead + 1, sort_words, (c, 0, 0, X_PASSES)))
-                waiting.append((ahead + 2, sort_words, (c, 1, 0, X_PASSES)))
-        for c in range(last):
+                waiting.append((ahead + 1, sort_words, (c, 0)))
+                waiting.append((ahead + 2, sort_words, (c, 1)))
+        for c in range(1, last):
             behind = TOKEN_TILES * (c + 1) + 1
             for m in range(TOKEN_TILES):
                 waiting.append((behind + m, group_h, (c, m, nc.scalar.copy)))
             if c + 1 < last:
                 waiting.append((behind + TOKEN_TILES, quantise_h, (c, 0, TOKENS)))
+        words_sorted = TOKEN_TILES * last - 3
+        for m in range(TOKEN_TILES):
+            waiting.append((words_sorted + 1 + m, group_h, (0, m, nc.vector.tensor_copy)))
+        waiting.append((words_sorted + 1 + TOKEN_TILES, quantise_h, (0, 0, TOKENS)))
+        waiting.append((TOKEN_TILES, move_rows, ()))
+        waiting.append((TOKEN_TILES, load_the_rest, ()))
 
         def issue_waiting(units_done):
             for due, work, arguments in waiting:
                 if due == units_done:
                     work(*arguments)
 
-        sort_first_planes(0, 0)
-        sort_words(0, 0, 0, 1)
-        quantise_x(TOKEN_TILES - 1)
-        sort_words(0, 0, 1, 2)
-        sort_first_planes(0, 1)
-        sort_words(0, 1, 0, X_PASSES)
         units_done = 0
         issue_waiting(units_done)
         for c in range(FF_CHUNKS):
@@ -360,8 +376,8 @@ def tile_mixllamamlp_kernel(
                 lhsT_scale=h_scales[:, g, m * P : (m + 1) * P],
                 rhs=down_words[g][:, columns].bitcast(FP8X4),
                 rhs_scale=plane,
-                start=(g == 0),
-                stop=(g == FF_CHUNKS - 1),
+                start=(g == down_order[0]),
+                stop=(g == down_order[-1]),
             )
 
         def store_bank(number, bank, m, columns):
@@ -380,7 +396,7 @@ def tile_mixllamamlp_kernel(
         for m, first, width in pieces[:together]:
             bank = banks.tile([P, width], F32, tag="bank", name="open_bank")
             open_banks.append(bank)
-        for g in range(FF_CHUNKS):
+        for g in down_order:
             for bank, (m, first, width) in zip(open_banks, pieces):
                 down_pass(bank, m, slice(first, first + width), g)
         for number, (m, first, width) in enumerate(pieces):
@@ -389,6 +405,6 @@ def tile_mixllamamlp_kernel(
                 bank = open_banks[number]
             else:
                 bank = banks.tile([P, width], F32, tag="bank", name="bank")
-                for g in range(FF_CHUNKS):
+                for g in down_order:
                     down_pass(bank, m, columns, g)
             store_bank(number, bank, m, columns)

@@ -28,6 +28,9 @@ OUT_HALVES = D_MODEL // N_TILE
 
 QUADRANTS = 4
 QUADRANT = 32
+STATIONARY_SCALES_AT = 64
+MOVING_CODES_AT = 128
+
 PLANE_ROWS = 4
 PLANES_PER_TILE = 4
 
@@ -59,6 +62,11 @@ def tile_mixllamamlp_kernel(
         banks = ctx.enter_context(tc.psum_pool(name="banks", bufs=8))
         ctx.enter_context(tc.manual_schedule())
 
+        def set_off(columns, dtype, item_bytes, start, name):
+            skipped = start // item_bytes
+            tile = resident.tile([P, skipped + columns], dtype, name=name, align_bytes=256)
+            return tile[:, skipped : skipped + columns]
+
         zeros = resident.tile([P, N_TILE], BF16, align_bytes=64)
         nc.vector.memset(zeros[:].bitcast(I32), 0)
         table_warmer = resident.tile([P, 1], F32)
@@ -68,11 +76,11 @@ def tile_mixllamamlp_kernel(
         early = FIRST_PLANES * K_PASS
         first_planes = []
         for w in range(2):
-            planes = resident.tile([P, early], U8, name="first_planes_%d" % w, align_bytes=64)
-            nc.vector.memset(planes[:].bitcast(I32), 0)
+            planes = set_off(early, U8, 1, STATIONARY_SCALES_AT, "first_planes_%d" % w)
+            nc.vector.memset(planes.bitcast(I32), 0)
             first_planes.append(planes)
         gate_up_planes = resident.tile([P, D_FF - early], U8, align_bytes=64)
-        down_planes = resident.tile([P, 2, D_MODEL], U8, align_bytes=64)
+        down_planes = resident.tile([P, 2, D_MODEL], U8, align_bytes=256)
         nc.vector.memset(gate_up_planes[:].bitcast(I32), 0)
         nc.vector.memset(down_planes[:].rearrange("p s n -> p (s n)").bitcast(I32), 0)
 
@@ -91,7 +99,7 @@ def tile_mixllamamlp_kernel(
             words = (W_gate_words, W_up_words)[w]
             if first_pass == 0:
                 raw_words[c, w] = resident.tile(
-                    [P, X_PASSES, K_PASS], I32, name="raw_words_%d_%d" % (c, w), align_bytes=64
+                    [P, X_PASSES, K_PASS], I32, name="raw_words_%d_%d" % (c, w), align_bytes=256
                 )
             nc.sync.dma_start(
                 out=raw_words[c, w][:, first_pass:end_pass, :],
@@ -122,8 +130,8 @@ def tile_mixllamamlp_kernel(
             for w in range(2):
                 load_raw_words(c, w, 0, 2)
 
-        x_codes = resident.tile([P, X_PASSES, TOKENS], U32, align_bytes=64)
-        x_scales = resident.tile([P, X_PASSES, TOKENS], U8, align_bytes=64)
+        x_codes = set_off(X_PASSES * TOKENS, U32, 4, MOVING_CODES_AT, "x_codes").rearrange("p (g r) -> p g r", g=X_PASSES)
+        x_scales = resident.tile([P, X_PASSES, TOKENS], U8, align_bytes=256)
         x_grouped = {}
 
         def transpose_x(m):
@@ -173,12 +181,12 @@ def tile_mixllamamlp_kernel(
         sorted_words = {}
         first_sorted_planes = []
         for w in range(2):
-            planes = resident.tile([P, early - K_PASS], U8, name="first_sorted_planes_%d" % w, align_bytes=64)
+            planes = set_off(early - K_PASS, U8, 1, STATIONARY_SCALES_AT, "first_sorted_planes_%d" % w)
             first_sorted_planes.append(planes)
-        sorted_planes = resident.tile([P, D_FF - early], U8, align_bytes=64)
+        sorted_planes = set_off(D_FF - early, U8, 1, STATIONARY_SCALES_AT, "sorted_planes")
 
         def sort_words(c, w):
-            in_order = resident.tile([P, X_PASSES, K_PASS], I32, name="sorted_words_%d_%d" % (c, w), align_bytes=64)
+            in_order = resident.tile([P, X_PASSES, K_PASS], I32, name="sorted_words_%d_%d" % (c, w), align_bytes=256)
             nc.vector.tensor_copy(
                 out=in_order[:].rearrange("p g (t m) -> p g m t", t=PACK),
                 in_=raw_words[c, w][:].rearrange("p g (m t) -> p g m t", t=PACK),
@@ -193,7 +201,7 @@ def tile_mixllamamlp_kernel(
 
         def sort_first_planes(c, w):
             columns = slice(c * K_PASS, (c + 1) * K_PASS)
-            sort_plane_bytes(first_sorted_planes[w][:], first_planes[w][:, columns])
+            sort_plane_bytes(first_sorted_planes[w], first_planes[w][:, columns])
 
         def sort_planes(c):
             columns = slice((c - FIRST_PLANES) * K_PASS, (c - FIRST_PLANES + 1) * K_PASS)
@@ -211,8 +219,10 @@ def tile_mixllamamlp_kernel(
                 plane = sorted_planes[plane_start:P, first - early : first - early + P]
             return words[:, g, t * P : (t + 1) * P].bitcast(FP8X4), plane
 
-        h_codes = resident.tile([P, FF_CHUNKS, TOKENS], U32, align_bytes=64)
-        h_scales = resident.tile([P, FF_CHUNKS, TOKENS], U8, align_bytes=64)
+        h_codes = resident.tile([P, FF_CHUNKS, TOKENS], U32, align_bytes=256)
+        h_scales = set_off(FF_CHUNKS * TOKENS, U8, 1, STATIONARY_SCALES_AT, "h_scales").rearrange(
+            "p (c r) -> p c r", c=FF_CHUNKS
+        )
         h_grouped = {}
 
         last = FF_CHUNKS - 1
@@ -244,8 +254,8 @@ def tile_mixllamamlp_kernel(
                 )
 
             for g in down_order:
-                pass_words = resident.tile([P, D_MODEL], I32, name="down_words_%d" % g, align_bytes=64)
-                nc.sync.dma_start(out=pass_words[:], in_=W_down_words[g].rearrange("p n t -> p (n t)").bitcast(I32))
+                pass_words = set_off(D_MODEL, I32, 4, MOVING_CODES_AT, "down_words_%d" % g)
+                nc.sync.dma_start(out=pass_words, in_=W_down_words[g].rearrange("p n t -> p (n t)").bitcast(I32))
                 down_words[g] = pass_words
 
         def project_wide(w, c, t):

@@ -126,7 +126,7 @@ def tile_mixllamamlp_kernel(
         load_raw_words(1, 1, 0, 2)
         for w in range(2):
             load_planes(gate_up_planes, w, slice(early, D_FF))
-        for c in range(2, 4):
+        for c in range(2, FF_CHUNKS):
             for w in range(2):
                 load_raw_words(c, w, 0, 2)
 
@@ -239,9 +239,7 @@ def tile_mixllamamlp_kernel(
         down_order = [1, 2, 0, 3, 4]
         down_words = {}
 
-        def load_the_rest():
-            for w in range(2):
-                load_raw_words(last, w, 0, 2)
+        def load_down():
             for quadrant in range(QUADRANTS):
                 rows = slice(PLANE_ROWS * quadrant, PLANE_ROWS * (quadrant + 1))
                 nc.sync.dma_start(
@@ -309,6 +307,11 @@ def tile_mixllamamlp_kernel(
                 out=h_tile[:, t, :], in0=up_bank[:], in1=silu_gate[:], op=mybir.AluOpType.mult
             )
 
+        def gpsimd_copy(out, in_):
+            nc.gpsimd.tensor_scalar(
+                out=out, in0=in_, scalar1=1.0, scalar2=0.0, op0=mybir.AluOpType.mult, op1=mybir.AluOpType.add
+            )
+
         def group_h(c, m, copy):
             if m == 0:
                 h_grouped[c] = h_stage.tile([P, TOKENS, PACK], BF16, align_bytes=64, name="h_grouped")
@@ -341,12 +344,11 @@ def tile_mixllamamlp_kernel(
                 waiting.append((behind + m, group_h, (c, m, nc.scalar.copy)))
             if c + 1 < last:
                 waiting.append((behind + TOKEN_TILES, quantise_h, (c, 0, TOKENS)))
-        words_sorted = TOKEN_TILES * last - 3
         for m in range(TOKEN_TILES):
-            waiting.append((words_sorted + 1 + m, group_h, (0, m, nc.vector.tensor_copy)))
-        waiting.append((words_sorted + 1 + TOKEN_TILES, quantise_h, (0, 0, TOKENS)))
+            waiting.append((TOKEN_TILES * last + 1, group_h, (0, m, gpsimd_copy)))
+        waiting.append((TOKEN_TILES * FF_CHUNKS - 1, quantise_h, (0, 0, TOKENS)))
         waiting.append((TOKEN_TILES, move_rows, ()))
-        waiting.append((TOKEN_TILES, load_the_rest, ()))
+        waiting.append((TOKEN_TILES, load_down, ()))
 
         def issue_waiting(units_done):
             for due, work, arguments in waiting:
@@ -400,7 +402,7 @@ def tile_mixllamamlp_kernel(
 
         pieces = [(m, half * N_TILE, N_TILE) for m in range(TOKEN_TILES) for half in range(OUT_HALVES)]
         m, first, width = pieces[-1]
-        pieces[-1:] = [(m, first, width // 2), (m, first + width // 2, width // 2)]
+        pieces[-1:] = [(m, first, width // 2), (m, first + width // 2, P), (m, first + width // 2 + P, P)]
         together = OPEN_TILES * OUT_HALVES
         open_banks = []
         for m, first, width in pieces[:together]:

@@ -35,7 +35,7 @@ PLANE_ROWS = 4
 PLANES_PER_TILE = 4
 
 WARM_UP_BEFORE_X = 4
-WARM_UP_BEHIND_X = 3
+WARM_UP_BEHIND_X = 2
 
 OPEN_TILES = 2
 
@@ -134,16 +134,20 @@ def tile_mixllamamlp_kernel(
         x_scales = resident.tile([P, X_PASSES, TOKENS], U8, align_bytes=256)
         x_grouped = {}
 
+        x_split = {}
+
+        def split_x(m):
+            split = x_stage.tile([P, X_PASSES * 2, P], F32, name="split")
+            nc.vector.tensor_copy(
+                out=split[:].rearrange("p (g u) w -> p g u w", u=2),
+                in_=x_tiles[m][:].bitcast(F32).rearrange("p (g w u) -> p g u w", g=X_PASSES, u=2),
+            )
+            x_split[m] = split
+
         def transpose_x(m):
-            x_words = x_tiles[m][:].bitcast(F32)
             bank = banks.tile([P, X_PASSES * 2, P], F32, tag="bank")
-            for g in range(X_PASSES):
-                for u in range(2):
-                    nc.tensor.transpose(
-                        out=bank[:, 2 * g + u, :],
-                        in_=x_words[:, 256 * g + u : 256 * (g + 1) : 2],
-                        identity=identity_f32[:],
-                    )
+            for half in range(X_PASSES * 2):
+                nc.tensor.transpose(out=bank[:, half, :], in_=x_split[m][:, half, :], identity=identity_f32[:])
             grouped = x_stage.tile([P, X_PASSES, P, PACK], BF16, align_bytes=64)
             grouped_words = (
                 grouped[:]
@@ -170,6 +174,8 @@ def tile_mixllamamlp_kernel(
                 nc.tensor.matmul(out=warm_bank[:], lhsT=zeros[:, 0:P], rhs=zeros[:], start=True, stop=True)
 
         warm_up(WARM_UP_BEFORE_X)
+        for m in range(TOKEN_TILES):
+            split_x(m)
         for m in range(TOKEN_TILES):
             transpose_x(m)
             warm_up(1)

@@ -336,6 +336,8 @@ def tile_mixllamamlp_kernel(
         waiting = []
         for c in range(1, FF_CHUNKS):
             ahead = TOKEN_TILES * c - 5
+            if c == FIRST_PLANES:
+                ahead += 1
             if c < FIRST_PLANES:
                 for w in range(2):
                     waiting.append((w, sort_first_planes, (c, w)))
@@ -365,13 +367,12 @@ def tile_mixllamamlp_kernel(
         issue_waiting(units_done)
         for c in range(FF_CHUNKS):
             h_sorted[c] = h_stage.tile([P, PACK, TOKENS], BF16, name="h_sorted")
-            if c == 0:
-                ready = first_gates()
+            ready = first_gates() if c == 0 else []
+            gate_run = 2 if c < 3 else 1
             for m in range(TOKEN_TILES):
-                if c == 0:
-                    wide_up(c, m, ready[m])
-                else:
-                    wide_up(c, m, wide_gate(c, m))
+                if c > 0 and m % gate_run == 0:
+                    ready[m:] = [wide_gate(c, t) for t in range(m, m + gate_run)]
+                wide_up(c, m, ready[m])
                 units_done += 1
                 issue_waiting(units_done)
 

from contextlib import ExitStack

import concourse.mybir as mybir
from concourse.masks import make_identity

BF16 = mybir.dt.bfloat16
F32 = mybir.dt.float32
I32 = mybir.dt.int32
U32 = mybir.dt.uint32
U8 = mybir.dt.uint8
FP8X4 = mybir.dt.float8_e4m3fn_x4

P = 128
PACK = 4
K_PASS = P * PACK
N_TILE = 512

TOKENS = 512
D_MODEL = 1024
D_FF = 2560

TOKEN_TILES = TOKENS // P
X_PASSES = D_MODEL // K_PASS
FF_CHUNKS = D_FF // K_PASS
TILES_PER_CHUNK = K_PASS // P
FEATURE_TILES = D_FF // P
OUT_HALVES = D_MODEL // N_TILE

QUADRANTS = 4
QUADRANT = 32
STATIONARY_SCALES_AT = 64
MOVING_CODES_AT = 128

PLANE_ROWS = 4
PLANES_PER_TILE = 4

WARM_UP_BEFORE_X = 4
WARM_UP_BEHIND_X = 2

OPEN_TILES = 2

FIRST_PLANES = 2

FIRST_MOVING = 256

FLOPS = 2 * TOKENS * D_MODEL * D_FF * 3


def tile_mixllamamlp_kernel(
    tc, x, W_gate_words, W_gate_scales, W_up_words, W_up_scales, W_down_words, W_down_scales, out
):
    nc = tc.nc
    x_rows = x.flatten_outer_dims()
    out_rows = out.flatten_outer_dims()

    with ExitStack() as ctx:
        resident = ctx.enter_context(tc.tile_pool(name="resident", bufs=1))
        x_stage = ctx.enter_context(tc.tile_pool(name="x_stage", bufs=4))
        silu_pool = ctx.enter_context(tc.tile_pool(name="silu_pool", bufs=4))
        h_stage = ctx.enter_context(tc.tile_pool(name="h_stage", bufs=5))
        y_pool = ctx.enter_context(tc.tile_pool(name="y_pool", bufs=8))
        banks = ctx.enter_context(tc.psum_pool(name="banks", bufs=8))
        ctx.enter_context(tc.manual_schedule())

        def set_off(columns, dtype, item_bytes, start, name):
            skipped = start // item_bytes
            tile = resident.tile([P, skipped + columns], dtype, name=name, align_bytes=256)
            return tile[:, skipped : skipped + columns]

        zeros = resident.tile([P, N_TILE], BF16, align_bytes=64)
        nc.vector.memset(zeros[:].bitcast(I32), 0)
        table_warmer = resident.tile([P, 1], F32)
        nc.vector.memset(table_warmer[:], 0.0)
        nc.scalar.activation(out=table_warmer[:], in_=table_warmer[:], func=mybir.ActivationFunctionType.Silu)

        early = FIRST_PLANES * K_PASS
        first_planes = []
        for w in range(2):
            planes = set_off(early, U8, 1, STATIONARY_SCALES_AT, "first_planes_%d" % w)
            nc.vector.memset(planes.bitcast(I32), 0)
            first_planes.append(planes)
        gate_up_planes = resident.tile([P, D_FF - early], U8, align_bytes=64)
        down_planes = resident.tile([P, 2, D_MODEL], U8, align_bytes=256)
        nc.vector.memset(gate_up_planes[:].bitcast(I32), 0)
        nc.vector.memset(down_planes[:].rearrange("p s n -> p (s n)").bitcast(I32), 0)

        identity_f32 = resident.tile([P, P], F32)
        make_identity(nc, identity_f32[:])

        x_tiles = []
        for m in range(TOKEN_TILES):
            x_tile = resident.tile([P, D_MODEL], BF16, name="x_tile_%d" % m)
            nc.sync.dma_start(out=x_tile[:], in_=x_rows[m * P : (m + 1) * P, :])
            x_tiles.append(x_tile)

        raw_words = {}

        def load_raw_words(c, w, first_pass, end_pass):
            words = (W_gate_words, W_up_words)[w]
            if first_pass == 0:
                raw_words[c, w] = resident.tile(
                    [P, X_PASSES, K_PASS], I32, name="raw_words_%d_%d" % (c, w), align_bytes=256
                )
            nc.sync.dma_start(
                out=raw_words[c, w][:, first_pass:end_pass, :],
                in_=words.rearrange("g p n t -> p g (n t)").bitcast(I32)[
                    :, first_pass:end_pass, c * K_PASS : (c + 1) * K_PASS
                ],
            )

        def load_planes(planes, w, columns):
            scales = (W_gate_scales, W_up_scales)[w]
            for quadrant in range(QUADRANTS):
                first = QUADRANT * quadrant + PLANE_ROWS * X_PASSES * w
                nc.sync.dma_start(
                    out=planes[first : first + PLANE_ROWS * X_PASSES, :].bitcast(I32),
                    in_=scales[:, PLANE_ROWS * quadrant : PLANE_ROWS * (quadrant + 1), columns].bitcast(I32),
                )

        load_planes(first_planes[0], 0, slice(0, early))
        load_raw_words(0, 0, 0, 1)
        load_raw_words(0, 0, 1, 2)
        load_planes(first_planes[1], 1, slice(0, early))
        load_raw_words(0, 1, 0, 2)
        load_raw_words(1, 0, 0, 2)
        load_raw_words(1, 1, 0, 2)
        for w in range(2):
            load_planes(gate_up_planes, w, slice(early, D_FF))
        for c in range(2, FF_CHUNKS):
            for w in range(2):
                load_raw_words(c, w, 0, 2)

        x_codes = set_off(X_PASSES * TOKENS, U32, 4, MOVING_CODES_AT, "x_codes").rearrange("p (g r) -> p g r", g=X_PASSES)
        x_scales = resident.tile([P, X_PASSES, TOKENS], U8, align_bytes=256)
        x_grouped = {}

        x_split = {}

        def split_x(m):
            split = x_stage.tile([P, X_PASSES * 2, P], F32, name="split")
            nc.vector.tensor_copy(
                out=split[:].rearrange("p (g u) w -> p g u w", u=2),
                in_=x_tiles[m][:].bitcast(F32).rearrange("p (g w u) -> p g u w", g=X_PASSES, u=2),
            )
            x_split[m] = split

        def transpose_x(m):
            bank = banks.tile([P, X_PASSES * 2, P], F32, tag="bank")
            for half in range(X_PASSES * 2):
                nc.tensor.transpose(out=bank[:, half, :], in_=x_split[m][:, half, :], identity=identity_f32[:])
            grouped = x_stage.tile([P, X_PASSES, P, PACK], BF16, align_bytes=64)
            grouped_words = (
                grouped[:]
                .rearrange("p g r t -> p (g r t)")
                .bitcast(F32)
                .rearrange("p (g r u) -> p g r u", g=X_PASSES, u=2)
            )
            transposed = bank[:].rearrange("p (g u) r -> p g r u", u=2)
            nc.scalar.copy(out=grouped_words, in_=transposed)
            x_grouped[m] = grouped

        def quantise_x(m):
            for g in range(X_PASSES):
                nc.vector.quantize_mx(
                    out=x_codes[:, g, m * P : (m + 1) * P].bitcast(FP8X4),
                    scales=x_scales[:, g, m * P : (m + 1) * P],
                    in_=x_grouped[m][:, g, :, :].rearrange("p r t -> p (r t)"),
                )

        warm_bank = banks.tile([P, N_TILE], F32, tag="bank")

        def warm_up(matmuls):
            for repeat in range(matmuls):
                nc.tensor.matmul(out=warm_bank[:], lhsT=zeros[:, 0:P], rhs=zeros[:], start=True, stop=True)

        warm_up(WARM_UP_BEFORE_X)
        for m in range(TOKEN_TILES):
            split_x(m)
        for m in range(TOKEN_TILES):
            transpose_x(m)
            warm_up(1)
            if m > 0:
                quantise_x(m - 1)
        quantise_x(TOKEN_TILES - 1)
        warm_up(WARM_UP_BEHIND_X)

        sorted_words = {}
        first_sorted_planes = []
        for w in range(2):
            planes = set_off(early - K_PASS, U8, 1, STATIONARY_SCALES_AT, "first_sorted_planes_%d" % w)
            first_sorted_planes.append(planes)
        sorted_planes = set_off(D_FF - early, U8, 1, STATIONARY_SCALES_AT, "sorted_planes")

        def sort_words(c, w):
            in_order = resident.tile([P, X_PASSES, K_PASS], I32, name="sorted_words_%d_%d" % (c, w), align_bytes=256)
            nc.vector.tensor_copy(
                out=in_order[:].rearrange("p g (t m) -> p g m t", t=PACK),
                in_=raw_words[c, w][:].rearrange("p g (m t) -> p g m t", t=PACK),
            )
            sorted_words[c, w] = in_order

        def sort_plane_bytes(in_order, as_loaded):
            nc.vector.tensor_copy(
                out=in_order.rearrange("p (t m) -> p m t", t=PACK),
                in_=as_loaded.rearrange("p (m t) -> p m t", t=PACK),
            )

        def sort_first_planes(c, w):
            columns = slice(c * K_PASS, (c + 1) * K_PASS)
            sort_plane_bytes(first_sorted_planes[w], first_planes[w][:, columns])

        def sort_planes(c):
            columns = slice((c - FIRST_PLANES) * K_PASS, (c - FIRST_PLANES + 1) * K_PASS)
            sort_plane_bytes(sorted_planes[:, columns], gate_up_planes[:, columns])

        def stationary(w, c, g, t):
            plane_start = PLANE_ROWS * (X_PASSES * w + g)
            first = c * K_PASS + t * P
            words = raw_words[c, w] if c == 0 else sorted_words[c, w]
            if c == 0:
                plane = first_planes[w][plane_start:P, first : first + P]
            elif c < FIRST_PLANES:
                plane = first_sorted_planes[w][plane_start:P, first - K_PASS : first - K_PASS + P]
            else:
                plane = sorted_planes[plane_start:P, first - early : first - early + P]
            return words[:, g, t * P : (t + 1) * P].bitcast(FP8X4), plane

        h_codes = resident.tile([P, FF_CHUNKS, TOKENS], U32, align_bytes=256)
        h_scales = set_off(FF_CHUNKS * TOKENS, U8, 1, STATIONARY_SCALES_AT, "h_scales").rearrange(
            "p (c r) -> p c r", c=FF_CHUNKS
        )
        h_grouped = {}

        last = FF_CHUNKS - 1
        h_sorted = {}
        h_natural = resident.tile([P, TILES_PER_CHUNK, TOKENS], BF16)

        def move_rows():
            for j in range(TILES_PER_CHUNK):
                for t in range(PACK):
                    nc.sync.dma_start(
                        out=h_sorted[0][QUADRANT * j : QUADRANT * (j + 1), t, :], in_=h_natural[t:P:PACK, j, :]
                    )

        down_order = [1, 2, 0, 3, 4]
        down_words = {}

        def load_down():
            for quadrant in range(QUADRANTS):
                rows = slice(PLANE_ROWS * quadrant, PLANE_ROWS * (quadrant + 1))
                nc.sync.dma_start(
                    out=down_planes[QUADRANT * quadrant : QUADRANT * quadrant + PLANE_ROWS * PLANES_PER_TILE, 0, :].bitcast(I32),
                    in_=W_down_scales[0:PLANES_PER_TILE, rows, :].bitcast(I32),
                )
                nc.sync.dma_start(
                    out=down_planes[QUADRANT * quadrant : QUADRANT * quadrant + PLANE_ROWS, 1, :].bitcast(I32),
                    in_=W_down_scales[PLANES_PER_TILE, rows, :].bitcast(I32),
                )

            for g in down_order:
                pass_words = set_off(D_MODEL, I32, 4, MOVING_CODES_AT, "down_words_%d" % g)
                nc.sync.dma_start(out=pass_words, in_=W_down_words[g].rearrange("p n t -> p (n t)").bitcast(I32))
                down_words[g] = pass_words

        def project_wide(w, c, t):
            bank = banks.tile([P, TOKENS], F32, tag="bank")
            for g in range(X_PASSES):
                codes, plane = stationary(w, c, g, t)
                nc.tensor.matmul_mx(
                    out=bank[:],
                    lhsT=codes,
                    lhsT_scale=plane,
                    rhs=x_codes[:, g, :].bitcast(FP8X4),
                    rhs_scale=x_scales[:, g, :],
                    start=(g == 0),
                    stop=(g == X_PASSES - 1),
                )
            return bank

        def silu_of(gate_bank):
            silu_gate = silu_pool.tile([P, TOKENS], F32)
            nc.scalar.activation(out=silu_gate[:], in_=gate_bank[:], func=mybir.ActivationFunctionType.Silu)
            return silu_gate

        def wide_gate(c, t):
            return silu_of(project_wide(0, c, t))

        def first_gates():
            gate_banks = []
            for t in range(PACK):
                gate_bank = banks.tile([P, TOKENS], F32, tag="bank", name="gate_bank")
                gate_banks.append(gate_bank)
            for first in range(0, TOKENS, FIRST_MOVING):
                tokens = slice(first, first + FIRST_MOVING)
                for g in range(X_PASSES):
                    for t in range(PACK):
                        codes, plane = stationary(0, 0, g, t)
                        nc.tensor.matmul_mx(
                            out=gate_banks[t][:, tokens],
                            lhsT=codes,
                            lhsT_scale=plane,
                            rhs=x_codes[:, g, tokens].bitcast(FP8X4),
                            rhs_scale=x_scales[:, g, tokens],
                            start=(g == 0),
                            stop=(g == X_PASSES - 1),
                        )
            return [silu_of(gate_bank) for gate_bank in gate_banks]

        def wide_up(c, t, silu_gate):
            up_bank = project_wide(1, c, t)
            h_tile = h_natural if c == 0 else h_sorted[c]
            nc.vector.tensor_tensor(
                out=h_tile[:, t, :], in0=up_bank[:], in1=silu_gate[:], op=mybir.AluOpType.mult
            )

        def gpsimd_copy(out, in_):
            nc.gpsimd.tensor_scalar(
                out=out, in0=in_, scalar1=1.0, scalar2=0.0, op0=mybir.AluOpType.mult, op1=mybir.AluOpType.add
            )

        def group_h(c, m, copy):
            if m == 0:
                h_grouped[c] = h_stage.tile([P, TOKENS, PACK], BF16, align_bytes=64, name="h_grouped")
            copy(
                out=h_grouped[c][:, m * P : (m + 1) * P, :],
                in_=h_sorted[c][:, :, m * P : (m + 1) * P].rearrange("p t r -> p r t"),
            )

        def quantise_h(c, first, end):
            nc.vector.quantize_mx(
                out=h_codes[:, c, first:end].bitcast(FP8X4),
                scales=h_scales[:, c, first:end],
                in_=h_grouped[c][:, first:end, :].rearrange("p r t -> p (r t)"),
            )

        waiting = []
        for c in range(1, FF_CHUNKS):
            ahead = TOKEN_TILES * c - 5
            if c == FIRST_PLANES:
                ahead += 1
            if c < FIRST_PLANES:
                for w in range(2):
                    waiting.append((w, sort_first_planes, (c, w)))
                    waiting.append((w, sort_words, (c, w)))
            else:
                waiting.append((ahead, sort_planes, (c,)))
                waiting.append((ahead + 1, sort_words, (c, 0)))
                waiting.append((ahead + 2, sort_words, (c, 1)))
        for c in range(1, last):
            behind = TOKEN_TILES * (c + 1) + 1
            for m in range(TOKEN_TILES):
                waiting.append((behind + m, group_h, (c, m, nc.scalar.copy)))
            if c + 1 < last:
                waiting.append((behind + TOKEN_TILES, quantise_h, (c, 0, TOKENS)))
        for m in range(TOKEN_TILES):
            waiting.append((TOKEN_TILES * last + 1, group_h, (0, m, gpsimd_copy)))
        waiting.append((TOKEN_TILES * FF_CHUNKS - 1, quantise_h, (0, 0, TOKENS)))
        waiting.append((TOKEN_TILES, move_rows, ()))
        waiting.append((TOKEN_TILES, load_down, ()))

        def issue_waiting(units_done):
            for due, work, arguments in waiting:
                if due == units_done:
                    work(*arguments)

        units_done = 0
        issue_waiting(units_done)
        for c in range(FF_CHUNKS):
            h_sorted[c] = h_stage.tile([P, PACK, TOKENS], BF16, name="h_sorted")
            ready = first_gates() if c == 0 else []
            gate_run = 2 if c < 3 else 1
            for m in range(TOKEN_TILES):
                if c > 0 and m % gate_run == 0:
                    ready[m:] = [wide_gate(c, t) for t in range(m, m + gate_run)]
                wide_up(c, m, ready[m])
                units_done += 1
                issue_waiting(units_done)

        group_h(last, 0, nc.vector.tensor_copy)
        group_h(last, 1, nc.vector.tensor_copy)
        quantise_h(last - 1, 0, TOKENS)
        for m in range(TOKEN_TILES):
            quantise_h(last, m * P, (m + 1) * P)
            if m + 2 < TOKEN_TILES:
                group_h(last, m + 2, nc.vector.tensor_copy)

        def down_pass(bank, m, columns, g):
            if g < PLANES_PER_TILE:
                plane = down_planes[PLANE_ROWS * g : P, 0, columns]
            else:
                plane = down_planes[:, 1, columns]
            nc.tensor.matmul_mx(
                out=bank[:],
                lhsT=h_codes[:, g, m * P : (m + 1) * P].bitcast(FP8X4),
                lhsT_scale=h_scales[:, g, m * P : (m + 1) * P],
                rhs=down_words[g][:, columns].bitcast(FP8X4),
                rhs_scale=plane,
                start=(g == down_order[0]),
                stop=(g == down_order[-1]),
            )

        def store_bank(number, bank, m, columns):
            y_tile = y_pool.tile([P, columns.stop - columns.start], F32, name="y_tile")
            if number % 2 == 0:
                nc.vector.tensor_copy(out=y_tile[:], in_=bank[:])
            else:
                nc.scalar.copy(out=y_tile[:], in_=bank[:])
            nc.sync.dma_start(out=out_rows[m * P : (m + 1) * P, columns], in_=y_tile[:])

        pieces = [(m, half * N_TILE, N_TILE) for m in range(TOKEN_TILES) for half in range(OUT_HALVES)]
        m, first, width = pieces[-1]
        pieces[-1:] = [(m, first, width // 2), (m, first + width // 2, P), (m, first + width // 2 + P, P)]
        together = OPEN_TILES * OUT_HALVES
        open_banks = []
        for m, first, width in pieces[:together]:
            bank = banks.tile([P, width], F32, tag="bank", name="open_bank")
            open_banks.append(bank)
        for g in down_order:
            for bank, (m, first, width) in zip(open_banks, pieces):
                down_pass(bank, m, slice(first, first + width), g)
        for number, (m, first, width) in enumerate(pieces):
            columns = slice(first, first + width)
            if number < together:
                bank = open_banks[number]
            else:
                bank = banks.tile([P, width], F32, tag="bank", name="bank")
                for g in down_order:
                    down_pass(bank, m, columns, g)
            store_bank(number, bank, m, columns)
